import numpy as np
import ml_dtypes


def mxq(x, axis, fmt="e4m3"):
    dtype, down = {"e4m3": (ml_dtypes.float8_e4m3fn, 7), "e5m2": (ml_dtypes.float8_e5m2, 14)}[fmt]
    v = np.moveaxis(np.asarray(x, np.float32).astype(ml_dtypes.bfloat16).astype(np.float64), axis, -1)
    blocks = v.reshape(v.shape[:-1] + (-1, 32))
    amax = np.abs(blocks).max(-1, keepdims=True)
    byte = np.maximum(np.where(amax > 0, np.frexp(amax)[1] - 1 + 127, 0) - down, 1)
    scale = np.exp2(byte - 127.0)
    codes = (blocks / scale).astype(np.float32).astype(dtype).astype(np.float64)
    return np.moveaxis((codes * scale).reshape(v.shape), -1, axis)


WIDE = False


def mx_kscale(k):
    if not WIDE:
        return np.ones(k)
    levels = np.array([10, -10, 5, -5, 0])
    if k % 512:
        return np.exp2(np.random.permutation(np.resize(levels, k // 32))).repeat(32)
    a = np.empty((k // 512, 16))
    for p in range(k // 512):
        a[p, :8] = np.random.permutation(np.resize(levels, 8))
        for g in range(8):
            far = levels[np.abs(levels - a[p, g]) >= 10]
            a[p, g + 8] = far[np.random.randint(len(far))]
    return np.exp2(a.ravel()).repeat(32)


BF16 = ml_dtypes.bfloat16


def bf(x):
    return np.asarray(x, np.float32).astype(BF16)


def f64(x):
    return np.asarray(x).astype(np.float64)


B, N, E, L, A, H1, H2, G = 256, 8, 8, 384, 128, 1024, 1024, 8
D = L + A
EPS = 1e-5


def mish(v):
    return v * np.tanh(np.log(1.0 + np.exp(v)))


def layer_norm(v, gamma, beta):
    mu = v.mean(-1, keepdims=True)
    var = v.var(-1, keepdims=True)
    return (v - mu) / np.sqrt(var + EPS) * gamma + beta


def setup_inputs():
    s = mx_kscale(D)
    r = np.random.standard_normal
    return {"tokens": bf(r((B, N, D)) * s),
            "logits": bf(r((B, N, E))),
            "W1": bf(r((E, D, H1)) / np.sqrt(D) / s[:, None]),
            "b1": bf(0.1 * r((E, H1))),
            "g1": bf(1.0 + 0.1 * r((E, H1))),
            "be1": bf(0.1 * r((E, H1)))}


def reference(tokens, logits, W1, b1, g1, be1):
    tok, lg = f64(tokens), f64(logits)
    ex = np.exp(lg - lg.max(1, keepdims=True))
    disp = ex / ex.sum(1, keepdims=True)
    slot = sum(disp[:, n, :].T[:, :, None] * tok[None, :, n, :] for n in range(N))
    h = (mxq(slot, 2, "e4m3") @ mxq(f64(W1), 1, "e4m3")) + f64(b1)[:, None, :]
    h = mish(layer_norm(h, f64(g1)[:, None, :], f64(be1)[:, None, :]))
    return h.transpose(1, 0, 2)

@@ -1,0 +1,403 @@
+from contextlib import ExitStack
+
+import concourse.mybir as mybir
+from concourse.masks import make_identity
+
+F32 = mybir.dt.float32
+BF16 = mybir.dt.bfloat16
+U32 = mybir.dt.uint32
+U8 = mybir.dt.uint8
+FP8X4 = mybir.dt.float8_e4m3fn_x4
+ALU = mybir.AluOpType
+ACT = mybir.ActivationFunctionType
+AX = mybir.AxisListType
+
+P = 128
+B, NA, E, D, H = 256, 8, 8, 512, 1024
+G = 16
+GB = 16
+PACK = 4
+EPS = 1e-5
+EP = 6
+NV = E - EP
+NB = E // 2
+HS = 768
+HS_LATE = 512
+VECTOR_STATS_FROM = 3
+POOL_BATCHES = 3
+
+FLOPS = 2 * E * B * D * H + 2 * B * NA * E * D
+
+
+def tile_softmoedynamics_pa_kernel(tc, tokens, logits, W1, b1, g1, be1, out):
+    nc = tc.nc
+    with ExitStack() as ctx:
+        cst = ctx.enter_context(tc.tile_pool(name="cst", bufs=1))
+        xp = ctx.enter_context(tc.tile_pool(name="xp", bufs=6))
+        up = ctx.enter_context(tc.tile_pool(name="up", bufs=6))
+        tnp = ctx.enter_context(tc.tile_pool(name="tnp", bufs=1))
+        wrp = ctx.enter_context(tc.tile_pool(name="wrp", bufs=3))
+        wgp = ctx.enter_context(tc.tile_pool(name="wgp", bufs=2))
+        wcp = ctx.enter_context(tc.tile_pool(name="wcp", bufs=5))
+        acp = ctx.enter_context(tc.tile_pool(name="acp", bufs=1))
+        stp = ctx.enter_context(tc.tile_pool(name="stp", bufs=8))
+        psH = ctx.enter_context(tc.psum_pool(name="psH", bufs=4))
+        psG = ctx.enter_context(tc.psum_pool(name="psG", bufs=2))
+        ctx.enter_context(tc.manual_schedule())
+
+        ident = cst.tile([P, P], F32, name="ident")
+        make_identity(nc, ident[:])
+        identb = cst.tile([P, P], BF16, name="identb")
+        make_identity(nc, identb[:])
+        mhalf = cst.tile([P, 4], F32, name="mhalf")
+        nc.gpsimd.memset(mhalf[:], -0.5)
+        warm = cst.tile([P, 1], F32, name="warm")
+        nc.vector.memset(warm[:], 0.0)
+        nc.scalar.activation(out=warm[:], in_=warm[:], func=ACT.Exp)
+
+        lg_raw = cst.tile([P, G, 16], BF16, name="lg_raw")
+        nc.sync.dma_start(out=lg_raw[:, :, 0:E], in_=logits.rearrange("(g b) n e -> (b n) g e", b=GB))
+        rows = cst.tile([P, P], BF16, name="rows")
+        nc.sync.dma_start(out=rows[0:64, :], in_=g1.rearrange("e (c q) -> (e c) q", q=P))
+        nc.sync.dma_start(out=rows[64:128, :], in_=be1.rearrange("e (c q) -> (e c) q", q=P))
+        lgn = cst.tile([P, 2, NA * E], BF16, name="lgn")
+        nc.sync.dma_start(out=lgn[:], in_=logits.rearrange("(t b) n e -> b t (n e)", b=P))
+        tok_view = tokens.rearrange("(g b) n d -> (b n) g d", b=GB)
+        trs = []
+        for q in range(4):
+            tr = up.tile([P, 4, D], BF16, tag="u", name="tr%d" % q)
+            nc.sync.dma_start(out=tr[:], in_=tok_view[:, 4 * q:4 * q + 4, :])
+            trs.append(tr)
+
+        wrs, wcs, wss, tns = {}, {}, {}, {}
+
+        def load_weights(e):
+            wrs[e] = wrp.tile([P, PACK, H], BF16, tag="wr", name="wr%d" % e)
+            nc.sync.dma_start(out=wrs[e][:], in_=W1[e].rearrange("(p j) h -> p j h", j=PACK))
+
+        bb = cst.tile([P, E, H], BF16, name="bb")
+
+        def load_bias(half):
+            nc.sync.dma_start(
+                out=bb[:, 4 * half:4 * half + 4, :].rearrange("p e h -> p (e h)"),
+                in_=b1[4 * half:4 * half + 4].rearrange("e h -> (e h)").partition_broadcast(P),
+            )
+
+        def load_tokens_by_batch(t):
+            tns[t] = tnp.tile([P, NA, D], BF16, tag="tn", name="tn%d" % t)
+            nc.sync.dma_start(out=tns[t][:], in_=tokens[P * t:P * t + P])
+
+        load_weights(0)
+        load_weights(1)
+        load_tokens_by_batch(0)
+        load_weights(2)
+
+        pgs, pbs = {}, {}
+
+        def spread(w, e):
+            dst = psG.tile([P, H], BF16, tag="pg%d" % w, name="pg%d_%d" % (w, e))
+            for c in range(8):
+                col = 64 * w + 8 * e + c
+                nc.tensor.transpose(dst[:, P * c:P * c + P], gcol[:, col:col + 1].to_broadcast([P, P]), identb[:])
+            (pgs, pbs)[w][e] = dst
+
+        mask = cst.tile([P, GB], F32, name="mask")
+        nc.vector.tensor_reduce(out=mask[:], in_=ident[:].rearrange("p (b n) -> p b n", n=NA), axis=AX.X, op=ALU.add)
+        lgf = cst.tile([P, G, E], F32, name="lgf")
+        nc.vector.tensor_copy(out=lgf[:], in_=lg_raw[:, :, 0:E])
+        psT = psH.tile([P, GB, NA], F32, tag="ph", name="psT")
+        nc.tensor.transpose(psT[:].rearrange("p b n -> p (b n)"), lgf[:].rearrange("p g e -> p (g e)"), ident[:])
+        psR = psH.tile([P, P], BF16, tag="ph", name="psR")
+        nc.tensor.transpose(psR[:], rows[:], identb[:])
+        mx = cst.tile([P, GB], F32, name="mx")
+        nc.vector.tensor_reduce(out=mx[:], in_=psT[:], axis=AX.X, op=ALU.max)
+        sh = cst.tile([P, GB, NA], F32, name="sh")
+        nc.vector.tensor_tensor(out=sh[:], in0=psT[:], in1=mx[:].unsqueeze(2).to_broadcast([P, GB, NA]), op=ALU.subtract)
+        nc.scalar.activation(out=sh[:], in_=sh[:], func=ACT.Exp)
+        gcol = cst.tile([P, P], BF16, name="gcol")
+        nc.vector.tensor_copy(out=gcol[:], in_=psR[:])
+        for e in range(2):
+            spread(0, e)
+            spread(1, e)
+
+        dn = cst.tile([P, 2, NV, NA], F32, name="dn")
+        dnv = dn[:].rearrange("b t e n -> b (t e) n")
+        nc.vector.tensor_copy(out=dn[:], in_=lgn[:].rearrange("b t (n e) -> b t e n", e=E)[:, :, EP:E, :])
+        mxn = cst.tile([P, 2 * NV], F32, name="mxn")
+        nc.vector.tensor_reduce(out=mxn[:], in_=dnv, axis=AX.X, op=ALU.max)
+        nc.vector.tensor_tensor(out=dnv, in0=dnv, in1=mxn[:].unsqueeze(2).to_broadcast([P, 2 * NV, NA]), op=ALU.subtract)
+        nc.scalar.activation(out=dnv, in_=dnv, func=ACT.Exp)
+
+        sm = cst.tile([P, GB], F32, name="sm")
+        nc.vector.tensor_reduce(out=sm[:], in_=sh[:], axis=AX.X, op=ALU.add)
+        rs = cst.tile([P, GB], F32, name="rs")
+        nc.vector.reciprocal(out=rs[:], in_=sm[:])
+        nc.vector.tensor_tensor(out=sh[:], in0=sh[:], in1=rs[:].unsqueeze(2).to_broadcast([P, GB, NA]), op=ALU.mult)
+        psD = psH.tile([P, G, E], F32, tag="ph", name="psD")
+        nc.tensor.transpose(psD[:].rearrange("p g e -> p (g e)"), sh[:].rearrange("p b n -> p (b n)"), ident[:])
+        smn = cst.tile([P, 2 * NV], F32, name="smn")
+        nc.vector.tensor_reduce(out=smn[:], in_=dnv, axis=AX.X, op=ALU.add)
+        rsn = cst.tile([P, 2 * NV], F32, name="rsn")
+        nc.vector.reciprocal(out=rsn[:], in_=smn[:])
+        nc.vector.tensor_tensor(out=dnv, in0=dnv, in1=rsn[:].unsqueeze(2).to_broadcast([P, 2 * NV, NA]), op=ALU.mult)
+
+        tfs = []
+        for q in range(4):
+            tf = xp.tile([P, 4, D], F32, tag="x", name="tf%d" % q)
+            tfs.append(tf)
+        dblk = cst.tile([P, G, EP, GB], F32, name="dblk")
+        for g0 in (0, 8):
+            nc.vector.tensor_tensor(
+                out=dblk[:, g0:g0 + 8, :, :],
+                in0=psD[:, g0:g0 + 8, 0:EP].unsqueeze(3).to_broadcast([P, 8, EP, GB]),
+                in1=mask[:].unsqueeze(1).unsqueeze(1).to_broadcast([P, 8, EP, GB]),
+                op=ALU.mult,
+            )
+            if g0 == 0:
+                nc.vector.tensor_copy(out=tfs[0][:], in_=trs[0][:])
+        for q in range(1, 4):
+            nc.scalar.copy(out=tfs[q][:], in_=trs[q][:])
+
+        wgs = {}
+
+        def regroup(e):
+            wgs[e] = wgp.tile([P, H, PACK], BF16, tag="wg", name="wg%d" % e, align_bytes=64)
+            hs = HS if e < 4 else HS_LATE
+            for copy_fn, c0, c1 in ((nc.vector.tensor_copy, 0, hs), (nc.scalar.copy, hs, H)):
+                copy_fn(
+                    out=wgs[e][:, c0:c1, :].rearrange("p (c i) t -> p c t i", i=4),
+                    in_=wrs[e][:, :, c0:c1].rearrange("p t (c i) -> p c t i", i=4),
+                )
+            if e + 3 < E:
+                load_weights(e + 3)
+
+        def quantise_weights(e):
+            wcs[e] = wcp.tile([P, H], U32, tag="wc", name="wc%d" % e, align_bytes=64)
+            wss[e] = wcp.tile([P, H], U8, tag="ws", name="ws%d" % e, align_bytes=64)
+            nc.vector.quantize_mx(
+                out=wcs[e][:].bitcast(FP8X4), scales=wss[e][:], in_=wgs[e][:].rearrange("p h j -> p (h j)")
+            )
+
+        gs = cst.tile([P, E, B, PACK], BF16, name="gs", align_bytes=64)
+        sc = cst.tile([P, E, B], U32, name="sc", align_bytes=64)
+        ss = cst.tile([P, E, B], U8, name="ss", align_bytes=64)
+
+        def quantise_slots(k):
+            nc.vector.quantize_mx(
+                out=sc[:, 2 * k:2 * k + 2, :].rearrange("p e b -> p (e b)").bitcast(FP8X4),
+                scales=ss[:, 2 * k:2 * k + 2, :].rearrange("p e b -> p (e b)"),
+                in_=gs[:, 2 * k:2 * k + 2, :, :].rearrange("p e b j -> p (e b j)"),
+            )
+
+        accs = {}
+
+        def sum_step(t, n):
+            for i in range(NV):
+                if n == 0:
+                    accs[i] = acp.tile([P, D], F32, tag="acc%d" % i, name="acc%d_%d" % (t, i))
+                    nc.vector.tensor_scalar_mul(out=accs[i][:], in0=tns[t][:, 0, :], scalar1=dn[:, t, i, 0:1])
+                else:
+                    nc.vector.scalar_tensor_tensor(
+                        out=accs[i][:], in0=tns[t][:, n, :], scalar=dn[:, t, i, n:n + 1], in1=accs[i][:],
+                        op0=ALU.mult, op1=ALU.add,
+                    )
+
+        psts = {}
+
+        def sum_transpose(t):
+            for i in range(NV):
+                psts[i] = psH.tile([P, PACK, P], F32, tag="ph", name="pst%d_%d" % (t, i))
+                for j in range(PACK):
+                    nc.tensor.transpose(psts[i][:, j, :], accs[i][:].rearrange("p (q j) -> p j q", j=PACK)[:, j, :], ident[:])
+
+        def sum_store(t):
+            for i in range(NV):
+                nc.vector.tensor_copy(out=gs[:, EP + i, P * t:P * t + P, :], in_=psts[i][:].rearrange("p j b -> p b j"))
+
+        for g in range(G):
+            ps = psH.tile([P, PACK, EP * GB], F32, tag="ph", name="ps%d" % g)
+            for j in range(PACK):
+                nc.tensor.matmul(
+                    ps[:, j, :],
+                    lhsT=tfs[g // 4][:, g % 4, :].rearrange("p (q j) -> p j q", j=PACK)[:, j, :],
+                    rhs=dblk[:, g, :, :].rearrange("p e b -> p (e b)"),
+                    start=True,
+                    stop=True,
+                )
+            nc.scalar.copy(out=gs[:, 0:EP, GB * g:GB * g + GB, :], in_=ps[:].rearrange("p j (e b) -> p e b j", e=EP))
+            if g % 4 == 0:
+                regroup(g // 4)
+            if g % 4 == 2:
+                quantise_weights(g // 4)
+            if g % 8 == 4:
+                load_bias(g // 8)
+            if 4 <= g < 4 + NA:
+                sum_step(0, g - 4)
+        load_tokens_by_batch(1)
+        quantise_slots(0)
+
+        xs, us, negmus, vss, rstds, mvs = {}, {}, {}, {}, {}, {}
+        junk = cst.tile([P, H], BF16, name="junk")
+        out_v = out.rearrange("(t b) e h -> b t e h", b=P)
+
+        phs = {}
+
+        def multiply(e):
+            for t in range(2):
+                for hh in range(2):
+                    phs[(e, t, hh)] = psH.tile([P, 512], F32, tag="ph", name="ph%d_%d_%d" % (e, t, hh))
+                    nc.tensor.matmul_mx(
+                        out=phs[(e, t, hh)][:],
+                        lhsT=sc[:, e, P * t:P * t + P].bitcast(FP8X4),
+                        lhsT_scale=ss[:, e, P * t:P * t + P],
+                        rhs=wcs[e][:, 512 * hh:512 * hh + 512].bitcast(FP8X4),
+                        rhs_scale=wss[e][:, 512 * hh:512 * hh + 512],
+                        start=True,
+                        stop=True,
+                    )
+
+        def add_bias(e, t):
+            by_vector = e // 2 >= VECTOR_STATS_FROM
+            if t == 0:
+                xs[e] = xp.tile([P, 2, H], F32, tag="x", name="x%d" % e)
+            if t == 0 and not by_vector:
+                negmus[e] = stp.tile([P, 2], F32, tag="negmu", name="negmu%d" % e)
+            if not by_vector:
+                s01 = stp.tile([P, 2], F32, tag="s01", name="s01_%d_%d" % (e, t))
+            for hh in range(2):
+                nc.vector.scalar_tensor_tensor(
+                    out=xs[e][:, t, 512 * hh:512 * hh + 512],
+                    in0=phs[(e, t, hh)][:],
+                    scalar=1.0,
+                    in1=bb[:, e, 512 * hh:512 * hh + 512],
+                    op0=ALU.mult,
+                    op1=ALU.add,
+                    accum_out=None if by_vector else s01[:, hh:hh + 1],
+                )
+            if not by_vector:
+                nc.vector.tensor_scalar(
+                    out=negmus[e][:, t:t + 1], in0=s01[:, 0:1], scalar1=s01[:, 1:2], scalar2=-1.0 / H,
+                    op0=ALU.add, op1=ALU.mult,
+                )
+            else:
+                if e % 2 == 0 and t == 0:
+                    mvs[e // 2] = stp.tile([P, 4, 2], F32, tag="mv", name="mv%d" % (e // 2))
+                st6 = stp.tile([P, 2, 6], F32, tag="st6", name="st6_%d_%d" % (e, t))
+                for hh in range(2):
+                    nc.vector.bn_stats(out=st6[:, hh, :], in_=xs[e][:, t, 512 * hh:512 * hh + 512])
+                nc.vector.bn_aggr(out=mvs[e // 2][:, 2 * (e % 2) + t, :], in_=st6[:].rearrange("p a s -> p (a s)"))
+
+        def centre_times_gamma(e):
+            us[e] = up.tile([P, 2, H], F32, tag="u", name="u%d" % e)
+            for t in range(2):
+                if e // 2 >= VECTOR_STATS_FROM:
+                    nc.vector.scalar_tensor_tensor(
+                        out=us[e][:, t, :], in0=xs[e][:, t, :], scalar=mvs[e // 2][:, 2 * (e % 2) + t, 0:1], in1=pgs[e][:],
+                        op0=ALU.subtract, op1=ALU.mult,
+                    )
+                else:
+                    nc.vector.scalar_tensor_tensor(
+                        out=us[e][:, t, :], in0=xs[e][:, t, :], scalar=negmus[e][:, t:t + 1], in1=pgs[e][:],
+                        op0=ALU.add, op1=ALU.mult,
+                    )
+            if e + 2 < E:
+                spread(0, e + 2)
+
+        def sum_of_squares(k, i):
+            e = 2 * k + i
+            if k >= VECTOR_STATS_FROM:
+                return
+            if i == 0:
+                vss[k] = stp.tile([P, 4], F32, tag="vs", name="vs%d" % k)
+            for t in range(2):
+                nc.scalar.activation(
+                    out=junk[:], in_=xs[e][:, t, :], func=ACT.Square, bias=negmus[e][:, t:t + 1],
+                    accum_out=vss[k][:, 2 * i + t:2 * i + t + 1],
+                )
+
+        def inverse_deviation(k):
+            ve = stp.tile([P, 4], F32, tag="ve", name="ve%d" % k)
+            rstds[k] = stp.tile([P, 4], F32, tag="rstd", name="rstd%d" % k)
+            if k >= VECTOR_STATS_FROM:
+                nc.gpsimd.tensor_scalar(out=ve[:], in0=mvs[k][:, :, 1], scalar1=1.0, scalar2=EPS, op0=ALU.mult, op1=ALU.add)
+            else:
+                nc.gpsimd.tensor_scalar(out=ve[:], in0=vss[k][:], scalar1=1.0 / H, scalar2=EPS, op0=ALU.mult, op1=ALU.add)
+            nc.gpsimd.tensor_tensor(out=rstds[k][:], in0=ve[:], in1=mhalf[:], op=ALU.pow)
+
+        def scale_add_beta(k, i):
+            e = 2 * k + i
+            for t in range(2):
+                nc.vector.scalar_tensor_tensor(
+                    out=xs[e][:, t, :], in0=us[e][:, t, :], scalar=rstds[k][:, 2 * i + t:2 * i + t + 1], in1=pbs[e][:],
+                    op0=ALU.mult, op1=ALU.add,
+                )
+            if e + 2 < E:
+                spread(1, e + 2)
+
+        def flat(tl):
+            return tl[:].rearrange("p t h -> p (t h)")
+
+        def finish(k, i):
+            e = 2 * k + i
+            eng = nc.gpsimd if k < POOL_BATCHES else nc.vector
+            if k < NB - 1:
+                nc.scalar.activation(out=flat(us[e]), in_=flat(us[e]), func=ACT.Tanh)
+                for t in range(2):
+                    eng.tensor_tensor(out=us[e][:, t, :], in0=xs[e][:, t, :], in1=us[e][:, t, :], op=ALU.mult)
+                nc.sync.dma_start(out=out_v[:, :, e, :], in_=us[e][:])
+            else:
+                for t in range(2):
+                    nc.scalar.activation(out=us[e][:, t, :], in_=us[e][:, t, :], func=ACT.Tanh)
+                    eng.tensor_tensor(out=us[e][:, t, :], in0=xs[e][:, t, :], in1=us[e][:, t, :], op=ALU.mult)
+                    nc.sync.dma_start(out=out_v[:, t, e, :], in_=us[e][:, t, :])
+
+        def head(k):
+            add_bias(2 * k, 0)
+            add_bias(2 * k, 1)
+            multiply(2 * k + 1)
+            centre_times_gamma(2 * k)
+            add_bias(2 * k + 1, 0)
+            add_bias(2 * k + 1, 1)
+            centre_times_gamma(2 * k + 1)
+
+        multiply(0)
+        head(0)
+        quantise_slots(1)
+        for c in range(-1, NB):
+            if c + 2 < NB:
+                multiply(2 * (c + 2))
+            for i in range(2):
+                if c >= 0:
+                    nc.scalar.activation(out=flat(us[2 * c + i]), in_=flat(us[2 * c + i]), func=ACT.Ln, bias=1.0)
+                if c + 1 < NB:
+                    sum_of_squares(c + 1, i)
+            if c + 1 < NB:
+                inverse_deviation(c + 1)
+                for i in range(2):
+                    scale_add_beta(c + 1, i)
+            if c >= 0:
+                for i in range(2):
+                    finish(c, i)
+            if c + 1 < NB:
+                for i in range(2):
+                    e = 2 * (c + 1) + i
+                    nc.scalar.activation(out=flat(us[e]), in_=flat(xs[e]), func=ACT.Exp)
+            if c + 2 < NB:
+                head(c + 2)
+            if c + 3 < NB:
+                if c == -1:
+                    sum_transpose(0)
+                regroup(2 * (c + 3))
+                regroup(2 * (c + 3) + 1)
+                if c == -1:
+                    quantise_slots(2)
+                    sum_store(0)
+                for n in range(4 * (c + 1), 4 * (c + 1) + 4):
+                    sum_step(1, n)
+                if c == 0:
+                    sum_transpose(1)
+                quantise_weights(2 * (c + 3))
+                quantise_weights(2 * (c + 3) + 1)
+                if c == 0:
+                    sum_store(1)
+                    quantise_slots(3)

@@ -143,7 +143,7 @@ def tile_softmoedynamics_pa_kernel(tc, tokens, logits, W1, b1, g1, be1, out):
 
         tfs = []
         for q in range(4):
-            tf = xp.tile([P, 4, D], F32, tag="x", name="tf%d" % q)
+            tf = xp.tile([P, 4, PACK, P], F32, tag="x", name="tf%d" % q)
             tfs.append(tf)
         dblk = cst.tile([P, G, EP, GB], F32, name="dblk")
         for g0 in (0, 8):
@@ -154,9 +154,9 @@ def tile_softmoedynamics_pa_kernel(tc, tokens, logits, W1, b1, g1, be1, out):
                 op=ALU.mult,
             )
             if g0 == 0:
-                nc.vector.tensor_copy(out=tfs[0][:], in_=trs[0][:])
+                nc.vector.tensor_copy(out=tfs[0][:], in_=trs[0][:].rearrange("p i (q j) -> p i j q", j=PACK))
         for q in range(1, 4):
-            nc.scalar.copy(out=tfs[q][:], in_=trs[q][:])
+            nc.scalar.copy(out=tfs[q][:], in_=trs[q][:].rearrange("p i (q j) -> p i j q", j=PACK))
 
         wgs = {}
 
@@ -189,7 +189,7 @@ def tile_softmoedynamics_pa_kernel(tc, tokens, logits, W1, b1, g1, be1, out):
                 in_=gs[:, 2 * k:2 * k + 2, :, :].rearrange("p e b j -> p (e b j)"),
             )
 
-        accs = {}
+        accs, slots = {}, {}
 
         def sum_step(t, n):
             for i in range(NV):
@@ -197,8 +197,11 @@ def tile_softmoedynamics_pa_kernel(tc, tokens, logits, W1, b1, g1, be1, out):
                     accs[i] = acp.tile([P, D], F32, tag="acc%d" % i, name="acc%d_%d" % (t, i))
                     nc.vector.tensor_scalar_mul(out=accs[i][:], in0=tns[t][:, 0, :], scalar1=dn[:, t, i, 0:1])
                 else:
+                    if n == NA - 1:
+                        slots[i] = acp.tile([P, D], BF16, tag="slot%d" % i, name="slot%d_%d" % (t, i))
                     nc.vector.scalar_tensor_tensor(
-                        out=accs[i][:], in0=tns[t][:, n, :], scalar=dn[:, t, i, n:n + 1], in1=accs[i][:],
+                        out=(slots if n == NA - 1 else accs)[i][:],
+                        in0=tns[t][:, n, :], scalar=dn[:, t, i, n:n + 1], in1=accs[i][:],
                         op0=ALU.mult, op1=ALU.add,
                     )
 
@@ -206,20 +209,23 @@ def tile_softmoedynamics_pa_kernel(tc, tokens, logits, W1, b1, g1, be1, out):
 
         def sum_transpose(t):
             for i in range(NV):
-                psts[i] = psH.tile([P, PACK, P], F32, tag="ph", name="pst%d_%d" % (t, i))
-                for j in range(PACK):
-                    nc.tensor.transpose(psts[i][:, j, :], accs[i][:].rearrange("p (q j) -> p j q", j=PACK)[:, j, :], ident[:])
+                psts[i] = psH.tile([P, 2, P], F32, tag="ph", name="pst%d_%d" % (t, i))
+                words = slots[i][:].bitcast(F32)
+                for u in range(2):
+                    nc.tensor.transpose(psts[i][:, u, :], words[:, u::2], ident[:])
 
         def sum_store(t):
             for i in range(NV):
-                nc.vector.tensor_copy(out=gs[:, EP + i, P * t:P * t + P, :], in_=psts[i][:].rearrange("p j b -> p b j"))
+                nc.vector.tensor_copy(
+                    out=gs[:, EP + i, P * t:P * t + P, :].bitcast(F32), in_=psts[i][:].rearrange("p u b -> p b u")
+                )
 
         for g in range(G):
             ps = psH.tile([P, PACK, EP * GB], F32, tag="ph", name="ps%d" % g)
             for j in range(PACK):
                 nc.tensor.matmul(
                     ps[:, j, :],
-                    lhsT=tfs[g // 4][:, g % 4, :].rearrange("p (q j) -> p j q", j=PACK)[:, j, :],
+                    lhsT=tfs[g // 4][:, g % 4, j, :],
                     rhs=dblk[:, g, :, :].rearrange("p e b -> p (e b)"),
                     start=True,
                     stop=True,

@@ -20,11 +20,18 @@ PACK = 4
 EPS = 1e-5
 EP = 6
 NV = E - EP
-NB = E // 2
-HS = 768
-HS_LATE = 512
-VECTOR_STATS_FROM = 3
-POOL_BATCHES = 3
+BATCHES = ((0,), (1, 2), (3, 4), (5, 6), (7,))
+BY_SCALAR = (0, 1, 2, 3, 4, 5)
+BY_POOL = (0, 1, 2, 3, 4, 5, 6)
+PB = ("S", "S", "G", "G")
+HS = (1024, 1024, 1024, 1024, 1024, 1024, 1024, 1024)
+SP = 256
+GP = 256
+REGROUPS = {-1: (), 0: (3,), 1: (4,), 2: (5,), 3: (6,), 4: (7,)}
+RB = ("V", "V", "V", "V", "V", "V", "V", "V")
+CB = ("V", "S", "S", "G")
+AHEAD = 2
+PREP = 3
 
 FLOPS = 2 * E * B * D * H + 2 * B * NA * E * D
 
@@ -34,15 +41,14 @@ def tile_softmoedynamics_pa_kernel(tc, tokens, logits, W1, b1, g1, be1, out):
     with ExitStack() as ctx:
         cst = ctx.enter_context(tc.tile_pool(name="cst", bufs=1))
         xp = ctx.enter_context(tc.tile_pool(name="xp", bufs=6))
-        up = ctx.enter_context(tc.tile_pool(name="up", bufs=6))
-        tnp = ctx.enter_context(tc.tile_pool(name="tnp", bufs=1))
+        up = ctx.enter_context(tc.tile_pool(name="up", bufs=7))
+        tnp = ctx.enter_context(tc.tile_pool(name="tnp", bufs=2))
         wrp = ctx.enter_context(tc.tile_pool(name="wrp", bufs=3))
         wgp = ctx.enter_context(tc.tile_pool(name="wgp", bufs=2))
-        wcp = ctx.enter_context(tc.tile_pool(name="wcp", bufs=5))
-        acp = ctx.enter_context(tc.tile_pool(name="acp", bufs=1))
+        wcp = ctx.enter_context(tc.tile_pool(name="wcp", bufs=3))
         stp = ctx.enter_context(tc.tile_pool(name="stp", bufs=8))
-        psH = ctx.enter_context(tc.psum_pool(name="psH", bufs=4))
-        psG = ctx.enter_context(tc.psum_pool(name="psG", bufs=2))
+        psH = ctx.enter_context(tc.psum_pool(name="psH", bufs=6))
+        psG = ctx.enter_context(tc.psum_pool(name="psG", bufs=1))
         ctx.enter_context(tc.manual_schedule())
 
         ident = cst.tile([P, P], F32, name="ident")
@@ -57,14 +63,10 @@ def tile_softmoedynamics_pa_kernel(tc, tokens, logits, W1, b1, g1, be1, out):
 
         lg_raw = cst.tile([P, G, 16], BF16, name="lg_raw")
         nc.sync.dma_start(out=lg_raw[:, :, 0:E], in_=logits.rearrange("(g b) n e -> (b n) g e", b=GB))
-        rows = cst.tile([P, P], BF16, name="rows")
-        nc.sync.dma_start(out=rows[0:64, :], in_=g1.rearrange("e (c q) -> (e c) q", q=P))
-        nc.sync.dma_start(out=rows[64:128, :], in_=be1.rearrange("e (c q) -> (e c) q", q=P))
-        lgn = cst.tile([P, 2, NA * E], BF16, name="lgn")
-        nc.sync.dma_start(out=lgn[:], in_=logits.rearrange("(t b) n e -> b t (n e)", b=P))
         tok_view = tokens.rearrange("(g b) n d -> (b n) g d", b=GB)
         trs = []
-        for q in range(4):
+
+        def load_tokens(q):
             tr = up.tile([P, 4, D], BF16, tag="u", name="tr%d" % q)
             nc.sync.dma_start(out=tr[:], in_=tok_view[:, 4 * q:4 * q + 4, :])
             trs.append(tr)
@@ -87,14 +89,27 @@ def tile_softmoedynamics_pa_kernel(tc, tokens, logits, W1, b1, g1, be1, out):
             tns[t] = tnp.tile([P, NA, D], BF16, tag="tn", name="tn%d" % t)
             nc.sync.dma_start(out=tns[t][:], in_=tokens[P * t:P * t + P])
 
+        load_tokens(0)
+        rows = cst.tile([P, P], BF16, name="rows")
+        nc.sync.dma_start(out=rows[0:64, :], in_=g1.rearrange("e (c q) -> (e c) q", q=P))
+        nc.sync.dma_start(out=rows[64:128, :], in_=be1.rearrange("e (c q) -> (e c) q", q=P))
+        load_tokens(1)
         load_weights(0)
-        load_weights(1)
+        load_tokens(2)
+        lgn = cst.tile([P, 2, NA * E], BF16, name="lgn")
+        nc.sync.dma_start(out=lgn[:], in_=logits.rearrange("(t b) n e -> b t (n e)", b=P))
+        load_tokens(3)
         load_tokens_by_batch(0)
+        load_weights(1)
         load_weights(2)
+        load_bias(0)
+        load_tokens_by_batch(1)
 
         pgs, pbs = {}, {}
 
         def spread(w, e):
+            if e >= E:
+                return
             dst = psG.tile([P, H], BF16, tag="pg%d" % w, name="pg%d_%d" % (w, e))
             for c in range(8):
                 col = 64 * w + 8 * e + c
@@ -107,27 +122,11 @@ def tile_softmoedynamics_pa_kernel(tc, tokens, logits, W1, b1, g1, be1, out):
         nc.vector.tensor_copy(out=lgf[:], in_=lg_raw[:, :, 0:E])
         psT = psH.tile([P, GB, NA], F32, tag="ph", name="psT")
         nc.tensor.transpose(psT[:].rearrange("p b n -> p (b n)"), lgf[:].rearrange("p g e -> p (g e)"), ident[:])
-        psR = psH.tile([P, P], BF16, tag="ph", name="psR")
-        nc.tensor.transpose(psR[:], rows[:], identb[:])
         mx = cst.tile([P, GB], F32, name="mx")
         nc.vector.tensor_reduce(out=mx[:], in_=psT[:], axis=AX.X, op=ALU.max)
         sh = cst.tile([P, GB, NA], F32, name="sh")
         nc.vector.tensor_tensor(out=sh[:], in0=psT[:], in1=mx[:].unsqueeze(2).to_broadcast([P, GB, NA]), op=ALU.subtract)
         nc.scalar.activation(out=sh[:], in_=sh[:], func=ACT.Exp)
-        gcol = cst.tile([P, P], BF16, name="gcol")
-        nc.vector.tensor_copy(out=gcol[:], in_=psR[:])
-        for e in range(2):
-            spread(0, e)
-            spread(1, e)
-
-        dn = cst.tile([P, 2, NV, NA], F32, name="dn")
-        dnv = dn[:].rearrange("b t e n -> b (t e) n")
-        nc.vector.tensor_copy(out=dn[:], in_=lgn[:].rearrange("b t (n e) -> b t e n", e=E)[:, :, EP:E, :])
-        mxn = cst.tile([P, 2 * NV], F32, name="mxn")
-        nc.vector.tensor_reduce(out=mxn[:], in_=dnv, axis=AX.X, op=ALU.max)
-        nc.vector.tensor_tensor(out=dnv, in0=dnv, in1=mxn[:].unsqueeze(2).to_broadcast([P, 2 * NV, NA]), op=ALU.subtract)
-        nc.scalar.activation(out=dnv, in_=dnv, func=ACT.Exp)
-
         sm = cst.tile([P, GB], F32, name="sm")
         nc.vector.tensor_reduce(out=sm[:], in_=sh[:], axis=AX.X, op=ALU.add)
         rs = cst.tile([P, GB], F32, name="rs")
@@ -135,39 +134,52 @@ def tile_softmoedynamics_pa_kernel(tc, tokens, logits, W1, b1, g1, be1, out):
         nc.vector.tensor_tensor(out=sh[:], in0=sh[:], in1=rs[:].unsqueeze(2).to_broadcast([P, GB, NA]), op=ALU.mult)
         psD = psH.tile([P, G, E], F32, tag="ph", name="psD")
         nc.tensor.transpose(psD[:].rearrange("p g e -> p (g e)"), sh[:].rearrange("p b n -> p (b n)"), ident[:])
-        smn = cst.tile([P, 2 * NV], F32, name="smn")
-        nc.vector.tensor_reduce(out=smn[:], in_=dnv, axis=AX.X, op=ALU.add)
-        rsn = cst.tile([P, 2 * NV], F32, name="rsn")
-        nc.vector.reciprocal(out=rsn[:], in_=smn[:])
-        nc.vector.tensor_tensor(out=dnv, in0=dnv, in1=rsn[:].unsqueeze(2).to_broadcast([P, 2 * NV, NA]), op=ALU.mult)
+
+        psR = psH.tile([P, P], BF16, tag="ph", name="psR")
+        nc.tensor.transpose(psR[:], rows[:], identb[:])
 
         tfs = []
         for q in range(4):
             tf = xp.tile([P, 4, PACK, P], F32, tag="x", name="tf%d" % q)
             tfs.append(tf)
+
+        def pool_copy(out, in_):
+            nc.gpsimd.tensor_scalar(out=out, in0=in_, scalar1=1.0, scalar2=0.0, op0=ALU.mult, op1=ALU.add)
+
+        def cast(q):
+            copy_fn = {"V": nc.vector.tensor_copy, "S": nc.scalar.copy, "G": pool_copy}[CB[q]]
+            copy_fn(out=tfs[q][:], in_=trs[q][:].rearrange("p i (q j) -> p i j q", j=PACK))
+
         dblk = cst.tile([P, G, EP, GB], F32, name="dblk")
-        for g0 in (0, 8):
+
+        def spread_dispatch(g0, n):
             nc.vector.tensor_tensor(
-                out=dblk[:, g0:g0 + 8, :, :],
-                in0=psD[:, g0:g0 + 8, 0:EP].unsqueeze(3).to_broadcast([P, 8, EP, GB]),
-                in1=mask[:].unsqueeze(1).unsqueeze(1).to_broadcast([P, 8, EP, GB]),
+                out=dblk[:, g0:g0 + n, :, :],
+                in0=psD[:, g0:g0 + n, 0:EP].unsqueeze(3).to_broadcast([P, n, EP, GB]),
+                in1=mask[:].unsqueeze(1).unsqueeze(1).to_broadcast([P, n, EP, GB]),
                 op=ALU.mult,
             )
-            if g0 == 0:
-                nc.vector.tensor_copy(out=tfs[0][:], in_=trs[0][:].rearrange("p i (q j) -> p i j q", j=PACK))
-        for q in range(1, 4):
-            nc.scalar.copy(out=tfs[q][:], in_=trs[q][:].rearrange("p i (q j) -> p i j q", j=PACK))
+
+        spread_dispatch(0, 4)
+        cast(0)
+        cast(1)
+        spread_dispatch(4, 12)
+        cast(2)
+        cast(3)
+        gcol = cst.tile([P, P], BF16, name="gcol")
+        nc.vector.tensor_copy(out=gcol[:], in_=psR[:])
 
         wgs = {}
 
         def regroup(e):
             wgs[e] = wgp.tile([P, H, PACK], BF16, tag="wg", name="wg%d" % e, align_bytes=64)
-            hs = HS if e < 4 else HS_LATE
-            for copy_fn, c0, c1 in ((nc.vector.tensor_copy, 0, hs), (nc.scalar.copy, hs, H)):
-                copy_fn(
-                    out=wgs[e][:, c0:c1, :].rearrange("p (c i) t -> p c t i", i=4),
-                    in_=wrs[e][:, :, c0:c1].rearrange("p t (c i) -> p c t i", i=4),
-                )
+            pieces = [(pool_copy, c0, c0 + GP) for c0 in range(0, H, GP)] if RB[e] == "G" else [(nc.vector.tensor_copy, 0, HS[e])] + [(nc.scalar.copy, c0, c0 + SP) for c0 in range(HS[e], H, SP)]
+            for copy_fn, c0, c1 in pieces:
+                if c0 < c1:
+                    copy_fn(
+                        out=wgs[e][:, c0:c1, :].rearrange("p (c i) t -> p c t i", i=4),
+                        in_=wrs[e][:, :, c0:c1].rearrange("p t (c i) -> p c t i", i=4),
+                    )
             if e + 3 < E:
                 load_weights(e + 3)
 
@@ -182,71 +194,58 @@ def tile_softmoedynamics_pa_kernel(tc, tokens, logits, W1, b1, g1, be1, out):
         sc = cst.tile([P, E, B], U32, name="sc", align_bytes=64)
         ss = cst.tile([P, E, B], U8, name="ss", align_bytes=64)
 
-        def quantise_slots(k):
+        def quantise_slots(e0, e1):
             nc.vector.quantize_mx(
-                out=sc[:, 2 * k:2 * k + 2, :].rearrange("p e b -> p (e b)").bitcast(FP8X4),
-                scales=ss[:, 2 * k:2 * k + 2, :].rearrange("p e b -> p (e b)"),
-                in_=gs[:, 2 * k:2 * k + 2, :, :].rearrange("p e b j -> p (e b j)"),
+                out=sc[:, e0:e1, :].rearrange("p e b -> p (e b)").bitcast(FP8X4),
+                scales=ss[:, e0:e1, :].rearrange("p e b -> p (e b)"),
+                in_=gs[:, e0:e1, :, :].rearrange("p e b j -> p (e b j)"),
             )
 
-        accs, slots = {}, {}
+        dn = cst.tile([P, 2, NV, NA], F32, name="dn")
+        dnv = dn[:].rearrange("b t e n -> b (t e) n")
 
-        def sum_step(t, n):
-            for i in range(NV):
-                if n == 0:
-                    accs[i] = acp.tile([P, D], F32, tag="acc%d" % i, name="acc%d_%d" % (t, i))
-                    nc.vector.tensor_scalar_mul(out=accs[i][:], in0=tns[t][:, 0, :], scalar1=dn[:, t, i, 0:1])
-                else:
-                    if n == NA - 1:
-                        slots[i] = acp.tile([P, D], BF16, tag="slot%d" % i, name="slot%d_%d" % (t, i))
-                    nc.vector.scalar_tensor_tensor(
-                        out=(slots if n == NA - 1 else accs)[i][:],
-                        in0=tns[t][:, n, :], scalar=dn[:, t, i, n:n + 1], in1=accs[i][:],
-                        op0=ALU.mult, op1=ALU.add,
-                    )
+        def softmax_by_batch():
+            nc.vector.tensor_copy(out=dn[:], in_=lgn[:].rearrange("b t (n e) -> b t e n", e=E)[:, :, EP:E, :])
+            mxn = cst.tile([P, 2 * NV], F32, name="mxn")
+            nc.vector.tensor_reduce(out=mxn[:], in_=dnv, axis=AX.X, op=ALU.max)
+            nc.vector.tensor_tensor(out=dnv, in0=dnv, in1=mxn[:].unsqueeze(2).to_broadcast([P, 2 * NV, NA]), op=ALU.subtract)
+            nc.scalar.activation(out=dnv, in_=dnv, func=ACT.Exp)
+            smn = cst.tile([P, 2 * NV], F32, name="smn")
+            nc.vector.tensor_reduce(out=smn[:], in_=dnv, axis=AX.X, op=ALU.add)
+            rsn = cst.tile([P, 2 * NV], F32, name="rsn")
+            nc.vector.reciprocal(out=rsn[:], in_=smn[:])
+            nc.vector.tensor_tensor(out=dnv, in0=dnv, in1=rsn[:].unsqueeze(2).to_broadcast([P, 2 * NV, NA]), op=ALU.mult)
+
+        prods = {}
+
+        def product(t, i, n, by):
+            if n % 4 == 0:
+                prods[(t, i, n // 4)] = up.tile([P, 4, PACK, P], F32, tag="u", name="prod%d_%d_%d" % (t, i, n // 4))
+            dst, src = prods[(t, i, n // 4)][:, n % 4, :, :], tns[t][:, n, :].rearrange("p (q j) -> p j q", j=PACK)
+            if by == "G":
+                nc.gpsimd.tensor_scalar(out=dst, in0=src, scalar1=dn[:, t, i, n:n + 1], scalar2=0.0, op0=ALU.mult, op1=ALU.add)
+            elif by == "S":
+                nc.scalar.activation(out=dst, in_=src, func=ACT.Copy, scale=dn[:, t, i, n:n + 1])
+            else:
+                nc.vector.tensor_scalar_mul(out=dst, in0=src, scalar1=dn[:, t, i, n:n + 1])
 
         psts = {}
 
-        def sum_transpose(t):
-            for i in range(NV):
-                psts[i] = psH.tile([P, 2, P], F32, tag="ph", name="pst%d_%d" % (t, i))
-                words = slots[i][:].bitcast(F32)
-                for u in range(2):
-                    nc.tensor.transpose(psts[i][:, u, :], words[:, u::2], ident[:])
-
-        def sum_store(t):
-            for i in range(NV):
-                nc.vector.tensor_copy(
-                    out=gs[:, EP + i, P * t:P * t + P, :].bitcast(F32), in_=psts[i][:].rearrange("p u b -> p b u")
-                )
-
-        for g in range(G):
-            ps = psH.tile([P, PACK, EP * GB], F32, tag="ph", name="ps%d" % g)
+        def sum_products(t, i):
+            psts[(t, i)] = psH.tile([P, PACK, P], F32, tag="ph", name="pst%d_%d" % (t, i))
             for j in range(PACK):
-                nc.tensor.matmul(
-                    ps[:, j, :],
-                    lhsT=tfs[g // 4][:, g % 4, j, :],
-                    rhs=dblk[:, g, :, :].rearrange("p e b -> p (e b)"),
-                    start=True,
-                    stop=True,
-                )
-            nc.scalar.copy(out=gs[:, 0:EP, GB * g:GB * g + GB, :], in_=ps[:].rearrange("p j (e b) -> p e b j", e=EP))
-            if g % 4 == 0:
-                regroup(g // 4)
-            if g % 4 == 2:
-                quantise_weights(g // 4)
-            if g % 8 == 4:
-                load_bias(g // 8)
-            if 4 <= g < 4 + NA:
-                sum_step(0, g - 4)
-        load_tokens_by_batch(1)
-        quantise_slots(0)
+                for n in range(NA):
+                    nc.tensor.matmul(
+                        psts[(t, i)][:, j, :], lhsT=prods[(t, i, n // 4)][:, n % 4, j, :], rhs=ident[:],
+                        start=(n == 0), stop=(n == NA - 1), is_transpose=True,
+                    )
 
-        xs, us, negmus, vss, rstds, mvs = {}, {}, {}, {}, {}, {}
+        def store_sums(t, i):
+            nc.scalar.copy(out=gs[:, EP + i, P * t:P * t + P, :], in_=psts[(t, i)][:].rearrange("p j b -> p b j"))
+
+        xs, us, sums, negmus, vss, rstds, mvs, phs = {}, {}, {}, {}, {}, {}, {}, {}
         junk = cst.tile([P, H], BF16, name="junk")
         out_v = out.rearrange("(t b) e h -> b t e h", b=P)
-
-        phs = {}
 
         def multiply(e):
             for t in range(2):
@@ -262,91 +261,80 @@ def tile_softmoedynamics_pa_kernel(tc, tokens, logits, W1, b1, g1, be1, out):
                         stop=True,
                     )
 
-        def add_bias(e, t):
-            by_vector = e // 2 >= VECTOR_STATS_FROM
-            if t == 0:
-                xs[e] = xp.tile([P, 2, H], F32, tag="x", name="x%d" % e)
-            if t == 0 and not by_vector:
-                negmus[e] = stp.tile([P, 2], F32, tag="negmu", name="negmu%d" % e)
-            if not by_vector:
-                s01 = stp.tile([P, 2], F32, tag="s01", name="s01_%d_%d" % (e, t))
-            for hh in range(2):
-                nc.vector.scalar_tensor_tensor(
-                    out=xs[e][:, t, 512 * hh:512 * hh + 512],
-                    in0=phs[(e, t, hh)][:],
-                    scalar=1.0,
-                    in1=bb[:, e, 512 * hh:512 * hh + 512],
-                    op0=ALU.mult,
-                    op1=ALU.add,
-                    accum_out=None if by_vector else s01[:, hh:hh + 1],
-                )
-            if not by_vector:
-                nc.vector.tensor_scalar(
-                    out=negmus[e][:, t:t + 1], in0=s01[:, 0:1], scalar1=s01[:, 1:2], scalar2=-1.0 / H,
-                    op0=ALU.add, op1=ALU.mult,
-                )
-            else:
-                if e % 2 == 0 and t == 0:
-                    mvs[e // 2] = stp.tile([P, 4, 2], F32, tag="mv", name="mv%d" % (e // 2))
-                st6 = stp.tile([P, 2, 6], F32, tag="st6", name="st6_%d_%d" % (e, t))
+        def add_bias(e):
+            by_scalar = e in BY_SCALAR
+            xs[e] = xp.tile([P, 2, H], F32, tag="x", name="x%d" % e)
+            s01 = stp.tile([P, 2, 2], F32, tag="s01", name="s01_%d" % e)
+            for t in range(2):
                 for hh in range(2):
-                    nc.vector.bn_stats(out=st6[:, hh, :], in_=xs[e][:, t, 512 * hh:512 * hh + 512])
-                nc.vector.bn_aggr(out=mvs[e // 2][:, 2 * (e % 2) + t, :], in_=st6[:].rearrange("p a s -> p (a s)"))
+                    nc.vector.scalar_tensor_tensor(
+                        out=xs[e][:, t, 512 * hh:512 * hh + 512],
+                        in0=phs[(e, t, hh)][:],
+                        scalar=1.0,
+                        in1=bb[:, e, 512 * hh:512 * hh + 512],
+                        op0=ALU.mult,
+                        op1=ALU.add,
+                        accum_out=s01[:, t, hh:hh + 1] if by_scalar else None,
+                    )
+            sums[e] = s01
+
+        def statistics(e):
+            rstds[e] = stp.tile([P, 2], F32, tag="rstd", name="rstd%d" % e)
+            ve = stp.tile([P, 2], F32, tag="ve", name="ve%d" % e)
+            if e in BY_SCALAR:
+                negmus[e] = stp.tile([P, 2], F32, tag="negmu", name="negmu%d" % e)
+                for t in range(2):
+                    nc.scalar.activation(
+                        out=junk[:, 0:2], in_=sums[e][:, t, :], func=ACT.Copy, scale=-1.0 / H, accum_out=negmus[e][:, t:t + 1]
+                    )
+                vss[e] = stp.tile([P, 2], F32, tag="vs", name="vs%d" % e)
+                for t in range(2):
+                    nc.scalar.activation(
+                        out=junk[:], in_=xs[e][:, t, :], func=ACT.Square, bias=negmus[e][:, t:t + 1],
+                        accum_out=vss[e][:, t:t + 1],
+                    )
+                nc.gpsimd.tensor_scalar(out=ve[:], in0=vss[e][:], scalar1=1.0 / H, scalar2=EPS, op0=ALU.mult, op1=ALU.add)
+            else:
+                mvs[e] = stp.tile([P, 2, 2], F32, tag="mv", name="mv%d" % e)
+                st6 = stp.tile([P, 2, 2, 6], F32, tag="st6", name="st6_%d" % e)
+                for t in range(2):
+                    for hh in range(2):
+                        nc.vector.bn_stats(out=st6[:, t, hh, :], in_=xs[e][:, t, 512 * hh:512 * hh + 512])
+                for t in range(2):
+                    nc.vector.bn_aggr(out=mvs[e][:, t, :], in_=st6[:, t, :, :].rearrange("p a s -> p (a s)"))
+                nc.gpsimd.tensor_scalar(out=ve[:], in0=mvs[e][:, :, 1], scalar1=1.0, scalar2=EPS, op0=ALU.mult, op1=ALU.add)
+            nc.gpsimd.tensor_tensor(out=rstds[e][:], in0=ve[:], in1=mhalf[:, 0:2], op=ALU.pow)
 
         def centre_times_gamma(e):
-            us[e] = up.tile([P, 2, H], F32, tag="u", name="u%d" % e)
-            for t in range(2):
-                if e // 2 >= VECTOR_STATS_FROM:
-                    nc.vector.scalar_tensor_tensor(
-                        out=us[e][:, t, :], in0=xs[e][:, t, :], scalar=mvs[e // 2][:, 2 * (e % 2) + t, 0:1], in1=pgs[e][:],
-                        op0=ALU.subtract, op1=ALU.mult,
-                    )
-                else:
-                    nc.vector.scalar_tensor_tensor(
-                        out=us[e][:, t, :], in0=xs[e][:, t, :], scalar=negmus[e][:, t:t + 1], in1=pgs[e][:],
-                        op0=ALU.add, op1=ALU.mult,
-                    )
-            if e + 2 < E:
-                spread(0, e + 2)
-
-        def sum_of_squares(k, i):
-            e = 2 * k + i
-            if k >= VECTOR_STATS_FROM:
-                return
-            if i == 0:
-                vss[k] = stp.tile([P, 4], F32, tag="vs", name="vs%d" % k)
-            for t in range(2):
-                nc.scalar.activation(
-                    out=junk[:], in_=xs[e][:, t, :], func=ACT.Square, bias=negmus[e][:, t:t + 1],
-                    accum_out=vss[k][:, 2 * i + t:2 * i + t + 1],
-                )
-
-        def inverse_deviation(k):
-            ve = stp.tile([P, 4], F32, tag="ve", name="ve%d" % k)
-            rstds[k] = stp.tile([P, 4], F32, tag="rstd", name="rstd%d" % k)
-            if k >= VECTOR_STATS_FROM:
-                nc.gpsimd.tensor_scalar(out=ve[:], in0=mvs[k][:, :, 1], scalar1=1.0, scalar2=EPS, op0=ALU.mult, op1=ALU.add)
-            else:
-                nc.gpsimd.tensor_scalar(out=ve[:], in0=vss[k][:], scalar1=1.0 / H, scalar2=EPS, op0=ALU.mult, op1=ALU.add)
-            nc.gpsimd.tensor_tensor(out=rstds[k][:], in0=ve[:], in1=mhalf[:], op=ALU.pow)
-
-        def scale_add_beta(k, i):
-            e = 2 * k + i
             for t in range(2):
                 nc.vector.scalar_tensor_tensor(
-                    out=xs[e][:, t, :], in0=us[e][:, t, :], scalar=rstds[k][:, 2 * i + t:2 * i + t + 1], in1=pbs[e][:],
+                    out=xs[e][:, t, :], in0=xs[e][:, t, :],
+                    scalar=negmus[e][:, t:t + 1] if e in BY_SCALAR else mvs[e][:, t, 0:1], in1=pgs[e][:],
+                    op0=ALU.add if e in BY_SCALAR else ALU.subtract, op1=ALU.mult,
+                )
+            spread(0, e + 1)
+
+        def scale_add_beta(e):
+            for t in range(2):
+                nc.vector.scalar_tensor_tensor(
+                    out=xs[e][:, t, :], in0=xs[e][:, t, :], scalar=rstds[e][:, t:t + 1], in1=pbs[e][:],
                     op0=ALU.mult, op1=ALU.add,
                 )
-            if e + 2 < E:
-                spread(1, e + 2)
+            spread(1, e + 1)
 
         def flat(tl):
             return tl[:].rearrange("p t h -> p (t h)")
 
-        def finish(k, i):
-            e = 2 * k + i
-            eng = nc.gpsimd if k < POOL_BATCHES else nc.vector
-            if k < NB - 1:
+        def exponential(e):
+            us[e] = up.tile([P, 2, H], F32, tag="u", name="u%d" % e)
+            nc.scalar.activation(out=flat(us[e]), in_=flat(xs[e]), func=ACT.Exp)
+
+        def logarithm(e):
+            nc.scalar.activation(out=flat(us[e]), in_=flat(us[e]), func=ACT.Ln, bias=1.0)
+
+        def finish(e):
+            eng = nc.gpsimd if e in BY_POOL else nc.vector
+            if e != E - 1:
                 nc.scalar.activation(out=flat(us[e]), in_=flat(us[e]), func=ACT.Tanh)
                 for t in range(2):
                     eng.tensor_tensor(out=us[e][:, t, :], in0=xs[e][:, t, :], in1=us[e][:, t, :], op=ALU.mult)
@@ -357,53 +345,81 @@ def tile_softmoedynamics_pa_kernel(tc, tokens, logits, W1, b1, g1, be1, out):
                     eng.tensor_tensor(out=us[e][:, t, :], in0=xs[e][:, t, :], in1=us[e][:, t, :], op=ALU.mult)
                     nc.sync.dma_start(out=out_v[:, t, e, :], in_=us[e][:, t, :])
 
-        def head(k):
-            add_bias(2 * k, 0)
-            add_bias(2 * k, 1)
-            multiply(2 * k + 1)
-            centre_times_gamma(2 * k)
-            add_bias(2 * k + 1, 0)
-            add_bias(2 * k + 1, 1)
-            centre_times_gamma(2 * k + 1)
+        def slot_group(g):
+            ps = psH.tile([P, PACK, EP * GB], F32, tag="ph", name="ps%d" % g)
+            for j in range(PACK):
+                nc.tensor.matmul(
+                    ps[:, j, :],
+                    lhsT=tfs[g // 4][:, g % 4, j, :],
+                    rhs=dblk[:, g, :, :].rearrange("p e b -> p (e b)"),
+                    start=True,
+                    stop=True,
+                )
+            nc.scalar.copy(out=gs[:, 0:EP, GB * g:GB * g + GB, :], in_=ps[:].rearrange("p j (e b) -> p e b j", e=EP))
 
+        NBT = len(BATCHES)
+
+        def batch(c):
+            return BATCHES[c] if 0 <= c < NBT else ()
+
+        for g in range(G):
+            slot_group(g)
+            if g == 1:
+                softmax_by_batch()
+                regroup(0)
+            if g == 5:
+                quantise_weights(0)
+                regroup(1)
+            if g == 8:
+                quantise_weights(1)
+                regroup(2)
+            if g >= 8:
+                product(0, 0, g - 8, PB[0])
+        load_bias(1)
+        quantise_slots(0, 2)
+        quantise_weights(2)
+        for n in range(NA):
+            product(0, 1, n, PB[1])
+        sum_products(0, 0)
         multiply(0)
-        head(0)
-        quantise_slots(1)
-        for c in range(-1, NB):
-            if c + 2 < NB:
-                multiply(2 * (c + 2))
-            for i in range(2):
-                if c >= 0:
-                    nc.scalar.activation(out=flat(us[2 * c + i]), in_=flat(us[2 * c + i]), func=ACT.Ln, bias=1.0)
-                if c + 1 < NB:
-                    sum_of_squares(c + 1, i)
-            if c + 1 < NB:
-                inverse_deviation(c + 1)
-                for i in range(2):
-                    scale_add_beta(c + 1, i)
-            if c >= 0:
-                for i in range(2):
-                    finish(c, i)
-            if c + 1 < NB:
-                for i in range(2):
-                    e = 2 * (c + 1) + i
-                    nc.scalar.activation(out=flat(us[e]), in_=flat(xs[e]), func=ACT.Exp)
-            if c + 2 < NB:
-                head(c + 2)
-            if c + 3 < NB:
-                if c == -1:
-                    sum_transpose(0)
-                regroup(2 * (c + 3))
-                regroup(2 * (c + 3) + 1)
-                if c == -1:
-                    quantise_slots(2)
-                    sum_store(0)
-                for n in range(4 * (c + 1), 4 * (c + 1) + 4):
-                    sum_step(1, n)
-                if c == 0:
-                    sum_transpose(1)
-                quantise_weights(2 * (c + 3))
-                quantise_weights(2 * (c + 3) + 1)
-                if c == 0:
-                    sum_store(1)
-                    quantise_slots(3)
+        spread(0, 0)
+        spread(1, 0)
+        add_bias(0)
+        multiply(1)
+        store_sums(0, 0)
+        statistics(0)
+        add_bias(1)
+        for n in range(NA):
+            product(1, 0, n, PB[2])
+        statistics(1)
+        sum_products(0, 1)
+        store_sums(0, 1)
+        quantise_slots(2, 4)
+        for e in REGROUPS[-1]:
+            regroup(e)
+        for c in range(NBT):
+            for k in batch(c):
+                centre_times_gamma(k)
+                scale_add_beta(k)
+                exponential(k)
+                for e in REGROUPS.get(k, ()):
+                    regroup(e)
+                if k == 0:
+                    quantise_slots(4, 6)
+                    for n in range(NA):
+                        product(1, 1, n, PB[3])
+                if k + AHEAD < E:
+                    multiply(k + AHEAD)
+                    add_bias(k + AHEAD)
+                    statistics(k + AHEAD)
+                if k < 2:
+                    sum_products(1, k)
+                    store_sums(1, k)
+                if k + PREP < E:
+                    quantise_weights(k + PREP)
+                if k == 2:
+                    quantise_slots(6, 8)
+            for k in batch(c):
+                logarithm(k)
+            for k in batch(c):
+                finish(k)

@@ -20,10 +20,10 @@ PACK = 4
 EPS = 1e-5
 EP = 6
 NV = E - EP
-BATCHES = ((0,), (1, 2), (3, 4), (5, 6), (7,))
-BY_SCALAR = (0, 1, 2, 3, 4, 5)
-BY_POOL = (0, 1, 2, 3, 4, 5, 6)
-PB = ("S", "S", "G", "G")
+BATCHES = ((0,), (1, 2), (3, 4), (5,), (6, 7))
+BY_SCALAR = (0, 1, 2, 3, 4)
+BY_POOL = (0, 1, 2, 3, 4, 5)
+PB = ("S", "S", "S", "S")
 HS = (1024, 1024, 1024, 1024, 1024, 1024, 1024, 1024)
 SP = 256
 GP = 256
@@ -399,6 +399,8 @@ def tile_softmoedynamics_pa_kernel(tc, tokens, logits, W1, b1, g1, be1, out):
             regroup(e)
         for c in range(NBT):
             for k in batch(c):
+                if k + AHEAD < E:
+                    multiply(k + AHEAD)
                 centre_times_gamma(k)
                 scale_add_beta(k)
                 exponential(k)
@@ -409,7 +411,6 @@ def tile_softmoedynamics_pa_kernel(tc, tokens, logits, W1, b1, g1, be1, out):
                     for n in range(NA):
                         product(1, 1, n, PB[3])
                 if k + AHEAD < E:
-                    multiply(k + AHEAD)
                     add_bias(k + AHEAD)
                     statistics(k + AHEAD)
                 if k < 2:

@@ -20,16 +20,17 @@ PACK = 4
 EPS = 1e-5
 EP = 6
 NV = E - EP
-BATCHES = ((0,), (1, 2), (3, 4), (5,), (6, 7))
+BATCHES = ((0, 1), (2,), (3, 4), (5,), (6, 7))
 BY_SCALAR = (0, 1, 2, 3, 4)
 BY_POOL = (0, 1, 2, 3, 4, 5)
 PB = ("S", "S", "S", "S")
 HS = (1024, 1024, 1024, 1024, 1024, 1024, 1024, 1024)
 SP = 256
 GP = 256
-REGROUPS = {-1: (), 0: (3,), 1: (4,), 2: (5,), 3: (6,), 4: (7,)}
+REGROUPS = {-1: (), 1: (4,), 2: (5,), 3: (6,), 4: (7,)}
 RB = ("V", "V", "V", "V", "V", "V", "V", "V")
-CB = ("V", "S", "S", "G")
+CB = ("V", "S", "S", "S")
+PS = (0, 0, 0, 0, 0, 1, 2, 3, 4, 5, 6, 8, 10, 12, 14, 15, 16)
 AHEAD = 2
 PREP = 3
 
@@ -45,7 +46,7 @@ def tile_softmoedynamics_pa_kernel(tc, tokens, logits, W1, b1, g1, be1, out):
         tnp = ctx.enter_context(tc.tile_pool(name="tnp", bufs=2))
         wrp = ctx.enter_context(tc.tile_pool(name="wrp", bufs=3))
         wgp = ctx.enter_context(tc.tile_pool(name="wgp", bufs=2))
-        wcp = ctx.enter_context(tc.tile_pool(name="wcp", bufs=3))
+        wcp = ctx.enter_context(tc.tile_pool(name="wcp", bufs=4))
         stp = ctx.enter_context(tc.tile_pool(name="stp", bufs=8))
         psH = ctx.enter_context(tc.psum_pool(name="psH", bufs=6))
         psG = ctx.enter_context(tc.psum_pool(name="psG", bufs=1))
@@ -89,21 +90,19 @@ def tile_softmoedynamics_pa_kernel(tc, tokens, logits, W1, b1, g1, be1, out):
             tns[t] = tnp.tile([P, NA, D], BF16, tag="tn", name="tn%d" % t)
             nc.sync.dma_start(out=tns[t][:], in_=tokens[P * t:P * t + P])
 
+        lgn = cst.tile([P, 2, NA * E], BF16, name="lgn")
+        nc.sync.dma_start(out=lgn[:], in_=logits.rearrange("(t b) n e -> b t (n e)", b=P))
         load_tokens(0)
         rows = cst.tile([P, P], BF16, name="rows")
         nc.sync.dma_start(out=rows[0:64, :], in_=g1.rearrange("e (c q) -> (e c) q", q=P))
         nc.sync.dma_start(out=rows[64:128, :], in_=be1.rearrange("e (c q) -> (e c) q", q=P))
         load_tokens(1)
-        load_weights(0)
         load_tokens(2)
-        lgn = cst.tile([P, 2, NA * E], BF16, name="lgn")
-        nc.sync.dma_start(out=lgn[:], in_=logits.rearrange("(t b) n e -> b t (n e)", b=P))
+        load_weights(0)
         load_tokens(3)
-        load_tokens_by_batch(0)
         load_weights(1)
+        load_tokens_by_batch(0)
         load_weights(2)
-        load_bias(0)
-        load_tokens_by_batch(1)
 
         pgs, pbs = {}, {}
 
@@ -127,13 +126,28 @@ def tile_softmoedynamics_pa_kernel(tc, tokens, logits, W1, b1, g1, be1, out):
         sh = cst.tile([P, GB, NA], F32, name="sh")
         nc.vector.tensor_tensor(out=sh[:], in0=psT[:], in1=mx[:].unsqueeze(2).to_broadcast([P, GB, NA]), op=ALU.subtract)
         nc.scalar.activation(out=sh[:], in_=sh[:], func=ACT.Exp)
+        dn = cst.tile([P, 2, NV, NA], F32, name="dn")
+        dnv = dn[:].rearrange("b t e n -> b (t e) n")
+        nc.vector.tensor_copy(out=dn[:], in_=lgn[:].rearrange("b t (n e) -> b t e n", e=E)[:, :, EP:E, :])
+        mxn = cst.tile([P, 2 * NV], F32, name="mxn")
+        nc.vector.tensor_reduce(out=mxn[:], in_=dnv, axis=AX.X, op=ALU.max)
         sm = cst.tile([P, GB], F32, name="sm")
         nc.vector.tensor_reduce(out=sm[:], in_=sh[:], axis=AX.X, op=ALU.add)
         rs = cst.tile([P, GB], F32, name="rs")
         nc.vector.reciprocal(out=rs[:], in_=sm[:])
+        nc.vector.tensor_tensor(out=dnv, in0=dnv, in1=mxn[:].unsqueeze(2).to_broadcast([P, 2 * NV, NA]), op=ALU.subtract)
+        nc.scalar.activation(out=dnv, in_=dnv, func=ACT.Exp)
         nc.vector.tensor_tensor(out=sh[:], in0=sh[:], in1=rs[:].unsqueeze(2).to_broadcast([P, GB, NA]), op=ALU.mult)
         psD = psH.tile([P, G, E], F32, tag="ph", name="psD")
         nc.tensor.transpose(psD[:].rearrange("p g e -> p (g e)"), sh[:].rearrange("p b n -> p (b n)"), ident[:])
+
+        smn = cst.tile([P, 2 * NV], F32, name="smn")
+        rsn = cst.tile([P, 2 * NV], F32, name="rsn")
+
+        def normalise_by_batch():
+            nc.vector.tensor_reduce(out=smn[:], in_=dnv, axis=AX.X, op=ALU.add)
+            nc.vector.reciprocal(out=rsn[:], in_=smn[:])
+            nc.vector.tensor_tensor(out=dnv, in0=dnv, in1=rsn[:].unsqueeze(2).to_broadcast([P, 2 * NV, NA]), op=ALU.mult)
 
         psR = psH.tile([P, P], BF16, tag="ph", name="psR")
         nc.tensor.transpose(psR[:], rows[:], identb[:])
@@ -201,21 +215,6 @@ def tile_softmoedynamics_pa_kernel(tc, tokens, logits, W1, b1, g1, be1, out):
                 in_=gs[:, e0:e1, :, :].rearrange("p e b j -> p (e b j)"),
             )
 
-        dn = cst.tile([P, 2, NV, NA], F32, name="dn")
-        dnv = dn[:].rearrange("b t e n -> b (t e) n")
-
-        def softmax_by_batch():
-            nc.vector.tensor_copy(out=dn[:], in_=lgn[:].rearrange("b t (n e) -> b t e n", e=E)[:, :, EP:E, :])
-            mxn = cst.tile([P, 2 * NV], F32, name="mxn")
-            nc.vector.tensor_reduce(out=mxn[:], in_=dnv, axis=AX.X, op=ALU.max)
-            nc.vector.tensor_tensor(out=dnv, in0=dnv, in1=mxn[:].unsqueeze(2).to_broadcast([P, 2 * NV, NA]), op=ALU.subtract)
-            nc.scalar.activation(out=dnv, in_=dnv, func=ACT.Exp)
-            smn = cst.tile([P, 2 * NV], F32, name="smn")
-            nc.vector.tensor_reduce(out=smn[:], in_=dnv, axis=AX.X, op=ALU.add)
-            rsn = cst.tile([P, 2 * NV], F32, name="rsn")
-            nc.vector.reciprocal(out=rsn[:], in_=smn[:])
-            nc.vector.tensor_tensor(out=dnv, in0=dnv, in1=rsn[:].unsqueeze(2).to_broadcast([P, 2 * NV, NA]), op=ALU.mult)
-
         prods = {}
 
         def product(t, i, n, by):
@@ -276,24 +275,23 @@ def tile_softmoedynamics_pa_kernel(tc, tokens, logits, W1, b1, g1, be1, out):
                         op1=ALU.add,
                         accum_out=s01[:, t, hh:hh + 1] if by_scalar else None,
                     )
-            sums[e] = s01
+            if by_scalar:
+                sums[e] = stp.tile([P, 2], F32, tag="sum", name="sum%d" % e)
+                nc.vector.tensor_reduce(out=sums[e][:], in_=s01[:], axis=AX.X, op=ALU.add)
 
         def statistics(e):
             rstds[e] = stp.tile([P, 2], F32, tag="rstd", name="rstd%d" % e)
             ve = stp.tile([P, 2], F32, tag="ve", name="ve%d" % e)
             if e in BY_SCALAR:
                 negmus[e] = stp.tile([P, 2], F32, tag="negmu", name="negmu%d" % e)
-                for t in range(2):
-                    nc.scalar.activation(
-                        out=junk[:, 0:2], in_=sums[e][:, t, :], func=ACT.Copy, scale=-1.0 / H, accum_out=negmus[e][:, t:t + 1]
-                    )
+                nc.gpsimd.tensor_scalar(out=negmus[e][:], in0=sums[e][:], scalar1=-1.0 / H, scalar2=0.0, op0=ALU.mult, op1=ALU.add)
                 vss[e] = stp.tile([P, 2], F32, tag="vs", name="vs%d" % e)
                 for t in range(2):
                     nc.scalar.activation(
-                        out=junk[:], in_=xs[e][:, t, :], func=ACT.Square, bias=negmus[e][:, t:t + 1],
+                        out=junk[:], in_=xs[e][:, t, :], func=ACT.Square, scale=-1.0 * H, bias=sums[e][:, t:t + 1],
                         accum_out=vss[e][:, t:t + 1],
                     )
-                nc.gpsimd.tensor_scalar(out=ve[:], in0=vss[e][:], scalar1=1.0 / H, scalar2=EPS, op0=ALU.mult, op1=ALU.add)
+                nc.gpsimd.tensor_scalar(out=ve[:], in0=vss[e][:], scalar1=1.0 / H ** 3, scalar2=EPS, op0=ALU.mult, op1=ALU.add)
             else:
                 mvs[e] = stp.tile([P, 2, 2], F32, tag="mv", name="mv%d" % e)
                 st6 = stp.tile([P, 2, 2, 6], F32, tag="st6", name="st6_%d" % e)
@@ -327,23 +325,22 @@ def tile_softmoedynamics_pa_kernel(tc, tokens, logits, W1, b1, g1, be1, out):
 
         def exponential(e):
             us[e] = up.tile([P, 2, H], F32, tag="u", name="u%d" % e)
-            nc.scalar.activation(out=flat(us[e]), in_=flat(xs[e]), func=ACT.Exp)
+            for t in range(2):
+                nc.scalar.activation(out=us[e][:, t, :], in_=xs[e][:, t, :], func=ACT.Exp)
 
         def logarithm(e):
             nc.scalar.activation(out=flat(us[e]), in_=flat(us[e]), func=ACT.Ln, bias=1.0)
 
         def finish(e):
             eng = nc.gpsimd if e in BY_POOL else nc.vector
-            if e != E - 1:
-                nc.scalar.activation(out=flat(us[e]), in_=flat(us[e]), func=ACT.Tanh)
-                for t in range(2):
-                    eng.tensor_tensor(out=us[e][:, t, :], in0=xs[e][:, t, :], in1=us[e][:, t, :], op=ALU.mult)
-                nc.sync.dma_start(out=out_v[:, :, e, :], in_=us[e][:])
-            else:
-                for t in range(2):
-                    nc.scalar.activation(out=us[e][:, t, :], in_=us[e][:, t, :], func=ACT.Tanh)
-                    eng.tensor_tensor(out=us[e][:, t, :], in0=xs[e][:, t, :], in1=us[e][:, t, :], op=ALU.mult)
-                    nc.sync.dma_start(out=out_v[:, t, e, :], in_=us[e][:, t, :])
+            pieces = 2 if e == E - 1 else 1
+            w = H // pieces
+            for t in range(2):
+                for d in range(pieces):
+                    cs = slice(d * w, (d + 1) * w)
+                    nc.scalar.activation(out=us[e][:, t, cs], in_=us[e][:, t, cs], func=ACT.Tanh)
+                    eng.tensor_tensor(out=us[e][:, t, cs], in0=xs[e][:, t, cs], in1=us[e][:, t, cs], op=ALU.mult)
+                    nc.sync.dma_start(out=out_v[:, t, e, cs], in_=us[e][:, t, cs])
 
         def slot_group(g):
             ps = psH.tile([P, PACK, EP * GB], F32, tag="ph", name="ps%d" % g)
@@ -362,37 +359,41 @@ def tile_softmoedynamics_pa_kernel(tc, tokens, logits, W1, b1, g1, be1, out):
         def batch(c):
             return BATCHES[c] if 0 <= c < NBT else ()
 
+        order = [(0, i, n) for i in range(NV) for n in range(NA)]
         for g in range(G):
             slot_group(g)
-            if g == 1:
-                softmax_by_batch()
+            if g == 0:
+                normalise_by_batch()
                 regroup(0)
+                load_bias(0)
+                load_tokens_by_batch(1)
             if g == 5:
                 quantise_weights(0)
                 regroup(1)
             if g == 8:
                 quantise_weights(1)
                 regroup(2)
-            if g >= 8:
-                product(0, 0, g - 8, PB[0])
+            for step in order[PS[g]:PS[g + 1]]:
+                product(*step, PB[0])
+        quantise_weights(2)
+        regroup(3)
         load_bias(1)
         quantise_slots(0, 2)
-        quantise_weights(2)
+        quantise_weights(3)
         for n in range(NA):
-            product(0, 1, n, PB[1])
-        sum_products(0, 0)
+            product(1, 0, n, PB[2])
         multiply(0)
         spread(0, 0)
         spread(1, 0)
         add_bias(0)
         multiply(1)
-        store_sums(0, 0)
         statistics(0)
         add_bias(1)
-        for n in range(NA):
-            product(1, 0, n, PB[2])
+        sum_products(0, 0)
         statistics(1)
+        store_sums(0, 0)
         sum_products(0, 1)
+        sum_products(1, 0)
         store_sums(0, 1)
         quantise_slots(2, 4)
         for e in REGROUPS[-1]:
@@ -407,16 +408,18 @@ def tile_softmoedynamics_pa_kernel(tc, tokens, logits, W1, b1, g1, be1, out):
                 for e in REGROUPS.get(k, ()):
                     regroup(e)
                 if k == 0:
+                    store_sums(1, 0)
                     quantise_slots(4, 6)
                     for n in range(NA):
                         product(1, 1, n, PB[3])
                 if k + AHEAD < E:
                     add_bias(k + AHEAD)
                     statistics(k + AHEAD)
-                if k < 2:
-                    sum_products(1, k)
-                    store_sums(1, k)
-                if k + PREP < E:
+                if k == 0:
+                    sum_products(1, 1)
+                if k == 1:
+                    store_sums(1, 1)
+                if 0 < k and k + PREP < E:
                     quantise_weights(k + PREP)
                 if k == 2:
                     quantise_slots(6, 8)

@@ -20,17 +20,18 @@ PACK = 4
 EPS = 1e-5
 EP = 6
 NV = E - EP
-BATCHES = ((0, 1), (2,), (3, 4), (5,), (6, 7))
+BATCHES = ((0, 1), (2, 3), (4, 5), (6, 7))
 BY_SCALAR = (0, 1, 2, 3, 4)
 BY_POOL = (0, 1, 2, 3, 4, 5)
 PB = ("S", "S", "S", "S")
-HS = (1024, 1024, 1024, 1024, 1024, 1024, 1024, 1024)
+HS = (1024, 1024, 1024, 0, 1024, 1024, 1024, 1024)
 SP = 256
 GP = 256
-REGROUPS = {-1: (), 1: (4,), 2: (5,), 3: (6,), 4: (7,)}
-RB = ("V", "V", "V", "V", "V", "V", "V", "V")
+LATER = {0: (5,), 1: (6,), 2: (7,)}
+REGROUPS = {-1: (4,), 0: (), 1: (), 2: (), 3: (), 4: ()}
+RB = ("V", "V", "V", "V", "G", "G", "G", "G")
 CB = ("V", "S", "S", "S")
-PS = (0, 0, 0, 0, 0, 1, 2, 3, 4, 5, 6, 8, 10, 12, 14, 15, 16)
+PS = (0, 0, 0, 0, 0, 1, 2, 3, 4, 5, 6, 7, 8, 9, 10, 11, 12)
 AHEAD = 2
 PREP = 3
 
@@ -42,11 +43,11 @@ def tile_softmoedynamics_pa_kernel(tc, tokens, logits, W1, b1, g1, be1, out):
     with ExitStack() as ctx:
         cst = ctx.enter_context(tc.tile_pool(name="cst", bufs=1))
         xp = ctx.enter_context(tc.tile_pool(name="xp", bufs=6))
-        up = ctx.enter_context(tc.tile_pool(name="up", bufs=7))
+        up = ctx.enter_context(tc.tile_pool(name="up", bufs=6))
         tnp = ctx.enter_context(tc.tile_pool(name="tnp", bufs=2))
         wrp = ctx.enter_context(tc.tile_pool(name="wrp", bufs=3))
-        wgp = ctx.enter_context(tc.tile_pool(name="wgp", bufs=2))
-        wcp = ctx.enter_context(tc.tile_pool(name="wcp", bufs=4))
+        wgp = ctx.enter_context(tc.tile_pool(name="wgp", bufs=3))
+        wcp = ctx.enter_context(tc.tile_pool(name="wcp", bufs=3))
         stp = ctx.enter_context(tc.tile_pool(name="stp", bufs=8))
         psH = ctx.enter_context(tc.psum_pool(name="psH", bufs=6))
         psG = ctx.enter_context(tc.psum_pool(name="psG", bufs=1))
@@ -103,6 +104,7 @@ def tile_softmoedynamics_pa_kernel(tc, tokens, logits, W1, b1, g1, be1, out):
         load_weights(1)
         load_tokens_by_batch(0)
         load_weights(2)
+        load_tokens_by_batch(1)
 
         pgs, pbs = {}, {}
 
@@ -219,7 +221,7 @@ def tile_softmoedynamics_pa_kernel(tc, tokens, logits, W1, b1, g1, be1, out):
 
         def product(t, i, n, by):
             if n % 4 == 0:
-                prods[(t, i, n // 4)] = up.tile([P, 4, PACK, P], F32, tag="u", name="prod%d_%d_%d" % (t, i, n // 4))
+                prods[(t, i, n // 4)] = (xp if t * i else up).tile([P, 4, PACK, P], F32, tag="x" if t * i else "u", name="prod%d_%d_%d" % (t, i, n // 4))
             dst, src = prods[(t, i, n // 4)][:, n % 4, :, :], tns[t][:, n, :].rearrange("p (q j) -> p j q", j=PACK)
             if by == "G":
                 nc.gpsimd.tensor_scalar(out=dst, in0=src, scalar1=dn[:, t, i, n:n + 1], scalar2=0.0, op0=ALU.mult, op1=ALU.add)
@@ -260,10 +262,14 @@ def tile_softmoedynamics_pa_kernel(tc, tokens, logits, W1, b1, g1, be1, out):
                         stop=True,
                     )
 
+        s01s, st6s = {}, {}
+
         def add_bias(e):
             by_scalar = e in BY_SCALAR
             xs[e] = xp.tile([P, 2, H], F32, tag="x", name="x%d" % e)
-            s01 = stp.tile([P, 2, 2], F32, tag="s01", name="s01_%d" % e)
+            if by_scalar:
+                s01s[e] = stp.tile([P, 2, 2], F32, tag="s01", name="s01_%d" % e)
+                sums[e] = stp.tile([P, 2], F32, tag="sum", name="sum%d" % e)
             for t in range(2):
                 for hh in range(2):
                     nc.vector.scalar_tensor_tensor(
@@ -273,11 +279,24 @@ def tile_softmoedynamics_pa_kernel(tc, tokens, logits, W1, b1, g1, be1, out):
                         in1=bb[:, e, 512 * hh:512 * hh + 512],
                         op0=ALU.mult,
                         op1=ALU.add,
-                        accum_out=s01[:, t, hh:hh + 1] if by_scalar else None,
+                        accum_out=s01s[e][:, t, hh:hh + 1] if by_scalar else None,
                     )
-            if by_scalar:
-                sums[e] = stp.tile([P, 2], F32, tag="sum", name="sum%d" % e)
-                nc.vector.tensor_reduce(out=sums[e][:], in_=s01[:], axis=AX.X, op=ALU.add)
+                    if by_scalar and (t, hh) == (1, 0):
+                        add_halves(e, 0)
+            if not by_scalar:
+                st6s[e] = stp.tile([P, 2, 2, 6], F32, tag="st6", name="st6_%d" % e)
+                mvs[e] = stp.tile([P, 2, 2], F32, tag="mv", name="mv%d" % e)
+                for t in range(2):
+                    for hh in range(2):
+                        nc.vector.bn_stats(out=st6s[e][:, t, hh, :], in_=xs[e][:, t, 512 * hh:512 * hh + 512])
+                        if (t, hh) == (1, 0):
+                            add_halves(e, 0)
+
+        def add_halves(e, t):
+            if e in BY_SCALAR:
+                nc.vector.tensor_reduce(out=sums[e][:, t:t + 1], in_=s01s[e][:, t, :], axis=AX.X, op=ALU.add)
+            else:
+                nc.vector.bn_aggr(out=mvs[e][:, t, :], in_=st6s[e][:, t, :, :].rearrange("p a s -> p (a s)"))
 
         def statistics(e):
             rstds[e] = stp.tile([P, 2], F32, tag="rstd", name="rstd%d" % e)
@@ -293,13 +312,6 @@ def tile_softmoedynamics_pa_kernel(tc, tokens, logits, W1, b1, g1, be1, out):
                     )
                 nc.gpsimd.tensor_scalar(out=ve[:], in0=vss[e][:], scalar1=1.0 / H ** 3, scalar2=EPS, op0=ALU.mult, op1=ALU.add)
             else:
-                mvs[e] = stp.tile([P, 2, 2], F32, tag="mv", name="mv%d" % e)
-                st6 = stp.tile([P, 2, 2, 6], F32, tag="st6", name="st6_%d" % e)
-                for t in range(2):
-                    for hh in range(2):
-                        nc.vector.bn_stats(out=st6[:, t, hh, :], in_=xs[e][:, t, 512 * hh:512 * hh + 512])
-                for t in range(2):
-                    nc.vector.bn_aggr(out=mvs[e][:, t, :], in_=st6[:, t, :, :].rearrange("p a s -> p (a s)"))
                 nc.gpsimd.tensor_scalar(out=ve[:], in0=mvs[e][:, :, 1], scalar1=1.0, scalar2=EPS, op0=ALU.mult, op1=ALU.add)
             nc.gpsimd.tensor_tensor(out=rstds[e][:], in0=ve[:], in1=mhalf[:, 0:2], op=ALU.pow)
 
@@ -332,13 +344,26 @@ def tile_softmoedynamics_pa_kernel(tc, tokens, logits, W1, b1, g1, be1, out):
             nc.scalar.activation(out=flat(us[e]), in_=flat(us[e]), func=ACT.Ln, bias=1.0)
 
         def finish(e):
+            tanh_only(e)
+            multiply_store(e)
+
+        def tanh_only(e):
+            pieces = 2 if e == E - 1 else 1
+            w = H // pieces
+            if e == E - 1:
+                return
+            for t in range(2):
+                nc.scalar.activation(out=us[e][:, t, :], in_=us[e][:, t, :], func=ACT.Tanh)
+
+        def multiply_store(e):
             eng = nc.gpsimd if e in BY_POOL else nc.vector
             pieces = 2 if e == E - 1 else 1
             w = H // pieces
             for t in range(2):
                 for d in range(pieces):
                     cs = slice(d * w, (d + 1) * w)
-                    nc.scalar.activation(out=us[e][:, t, cs], in_=us[e][:, t, cs], func=ACT.Tanh)
+                    if e == E - 1:
+                        nc.scalar.activation(out=us[e][:, t, cs], in_=us[e][:, t, cs], func=ACT.Tanh)
                     eng.tensor_tensor(out=us[e][:, t, cs], in0=xs[e][:, t, cs], in1=us[e][:, t, cs], op=ALU.mult)
                     nc.sync.dma_start(out=out_v[:, t, e, cs], in_=us[e][:, t, cs])
 
@@ -366,7 +391,6 @@ def tile_softmoedynamics_pa_kernel(tc, tokens, logits, W1, b1, g1, be1, out):
                 normalise_by_batch()
                 regroup(0)
                 load_bias(0)
-                load_tokens_by_batch(1)
             if g == 5:
                 quantise_weights(0)
                 regroup(1)
@@ -375,29 +399,35 @@ def tile_softmoedynamics_pa_kernel(tc, tokens, logits, W1, b1, g1, be1, out):
                 regroup(2)
             for step in order[PS[g]:PS[g + 1]]:
                 product(*step, PB[0])
+        for step in order[PS[G]:]:
+            product(*step, PB[0])
         quantise_weights(2)
-        regroup(3)
+        for i in range(NV):
+            for n in range(NA):
+                product(1, i, n, "V")
         load_bias(1)
         quantise_slots(0, 2)
-        quantise_weights(3)
-        for n in range(NA):
-            product(1, 0, n, PB[2])
+        regroup(3)
         multiply(0)
         spread(0, 0)
         spread(1, 0)
         add_bias(0)
         multiply(1)
+        quantise_slots(2, 4)
+        add_halves(0, 1)
         statistics(0)
         add_bias(1)
         sum_products(0, 0)
+        quantise_slots(4, 6)
+        add_halves(1, 1)
         statistics(1)
         store_sums(0, 0)
         sum_products(0, 1)
         sum_products(1, 0)
         store_sums(0, 1)
-        quantise_slots(2, 4)
         for e in REGROUPS[-1]:
             regroup(e)
+        pending = []
         for c in range(NBT):
             for k in batch(c):
                 if k + AHEAD < E:
@@ -409,21 +439,27 @@ def tile_softmoedynamics_pa_kernel(tc, tokens, logits, W1, b1, g1, be1, out):
                     regroup(e)
                 if k == 0:
                     store_sums(1, 0)
-                    quantise_slots(4, 6)
-                    for n in range(NA):
-                        product(1, 1, n, PB[3])
                 if k + AHEAD < E:
                     add_bias(k + AHEAD)
+                    if k + PREP < E:
+                        quantise_weights(k + PREP)
+                    add_halves(k + AHEAD, 1)
                     statistics(k + AHEAD)
+                while pending:
+                    multiply_store(pending.pop(0))
+                for e in LATER.get(k, ()):
+                    regroup(e)
                 if k == 0:
                     sum_products(1, 1)
                 if k == 1:
                     store_sums(1, 1)
-                if 0 < k and k + PREP < E:
-                    quantise_weights(k + PREP)
                 if k == 2:
                     quantise_slots(6, 8)
             for k in batch(c):
                 logarithm(k)
             for k in batch(c):
-                finish(k)
+                tanh_only(k)
+                if k == batch(c)[0] or c == NBT - 1:
+                    multiply_store(k)
+                else:
+                    pending.append(k)

from contextlib import ExitStack

import concourse.mybir as mybir
from concourse.masks import make_identity

F32 = mybir.dt.float32
BF16 = mybir.dt.bfloat16
U32 = mybir.dt.uint32
U8 = mybir.dt.uint8
FP8X4 = mybir.dt.float8_e4m3fn_x4
ALU = mybir.AluOpType
ACT = mybir.ActivationFunctionType
AX = mybir.AxisListType

P = 128
B, NA, E, D, H = 256, 8, 8, 512, 1024
G = 16
GB = 16
PACK = 4
EPS = 1e-5
EP = 6
NV = E - EP
BATCHES = ((0, 1), (2, 3), (4, 5), (6, 7))
BY_SCALAR = (0, 1, 2, 3, 4)
BY_POOL = (0, 1, 2, 3, 4, 5)
PB = ("S", "S", "S", "S")
HS = (1024, 1024, 1024, 0, 1024, 1024, 1024, 1024)
SP = 256
GP = 256
LATER = {0: (5,), 1: (6,), 2: (7,)}
REGROUPS = {-1: (4,), 0: (), 1: (), 2: (), 3: (), 4: ()}
RB = ("V", "V", "V", "V", "G", "G", "G", "G")
CB = ("V", "S", "S", "S")
PS = (0, 0, 0, 0, 0, 1, 2, 3, 4, 5, 6, 7, 8, 9, 10, 11, 12)
AHEAD = 2
PREP = 3

FLOPS = 2 * E * B * D * H + 2 * B * NA * E * D


def tile_softmoedynamics_pa_kernel(tc, tokens, logits, W1, b1, g1, be1, out):
    nc = tc.nc
    with ExitStack() as ctx:
        cst = ctx.enter_context(tc.tile_pool(name="cst", bufs=1))
        xp = ctx.enter_context(tc.tile_pool(name="xp", bufs=6))
        up = ctx.enter_context(tc.tile_pool(name="up", bufs=6))
        tnp = ctx.enter_context(tc.tile_pool(name="tnp", bufs=2))
        wrp = ctx.enter_context(tc.tile_pool(name="wrp", bufs=3))
        wgp = ctx.enter_context(tc.tile_pool(name="wgp", bufs=3))
        wcp = ctx.enter_context(tc.tile_pool(name="wcp", bufs=3))
        stp = ctx.enter_context(tc.tile_pool(name="stp", bufs=8))
        psH = ctx.enter_context(tc.psum_pool(name="psH", bufs=6))
        psG = ctx.enter_context(tc.psum_pool(name="psG", bufs=1))
        ctx.enter_context(tc.manual_schedule())

        ident = cst.tile([P, P], F32, name="ident")
        make_identity(nc, ident[:])
        identb = cst.tile([P, P], BF16, name="identb")
        make_identity(nc, identb[:])
        mhalf = cst.tile([P, 4], F32, name="mhalf")
        nc.gpsimd.memset(mhalf[:], -0.5)
        warm = cst.tile([P, 1], F32, name="warm")
        nc.vector.memset(warm[:], 0.0)
        nc.scalar.activation(out=warm[:], in_=warm[:], func=ACT.Exp)

        lg_raw = cst.tile([P, G, 16], BF16, name="lg_raw")
        nc.sync.dma_start(out=lg_raw[:, :, 0:E], in_=logits.rearrange("(g b) n e -> (b n) g e", b=GB))
        tok_view = tokens.rearrange("(g b) n d -> (b n) g d", b=GB)
        trs = []

        def load_tokens(q):
            tr = up.tile([P, 4, D], BF16, tag="u", name="tr%d" % q)
            nc.sync.dma_start(out=tr[:], in_=tok_view[:, 4 * q:4 * q + 4, :])
            trs.append(tr)

        wrs, wcs, wss, tns = {}, {}, {}, {}

        def load_weights(e):
            wrs[e] = wrp.tile([P, PACK, H], BF16, tag="wr", name="wr%d" % e)
            nc.sync.dma_start(out=wrs[e][:], in_=W1[e].rearrange("(p j) h -> p j h", j=PACK))

        bb = cst.tile([P, E, H], BF16, name="bb")

        def load_bias(half):
            nc.sync.dma_start(
                out=bb[:, 4 * half:4 * half + 4, :].rearrange("p e h -> p (e h)"),
                in_=b1[4 * half:4 * half + 4].rearrange("e h -> (e h)").partition_broadcast(P),
            )

        def load_tokens_by_batch(t):
            tns[t] = tnp.tile([P, NA, D], BF16, tag="tn", name="tn%d" % t)
            nc.sync.dma_start(out=tns[t][:], in_=tokens[P * t:P * t + P])

        lgn = cst.tile([P, 2, NA * E], BF16, name="lgn")
        nc.sync.dma_start(out=lgn[:], in_=logits.rearrange("(t b) n e -> b t (n e)", b=P))
        load_tokens(0)
        rows = cst.tile([P, P], BF16, name="rows")
        nc.sync.dma_start(out=rows[0:64, :], in_=g1.rearrange("e (c q) -> (e c) q", q=P))
        nc.sync.dma_start(out=rows[64:128, :], in_=be1.rearrange("e (c q) -> (e c) q", q=P))
        load_tokens(1)
        load_tokens(2)
        load_weights(0)
        load_tokens(3)
        load_weights(1)
        load_tokens_by_batch(0)
        load_weights(2)
        load_tokens_by_batch(1)

        pgs, pbs = {}, {}

        def spread(w, e):
            if e >= E:
                return
            dst = psG.tile([P, H], BF16, tag="pg%d" % w, name="pg%d_%d" % (w, e))
            for c in range(8):
                col = 64 * w + 8 * e + c
                nc.tensor.transpose(dst[:, P * c:P * c + P], gcol[:, col:col + 1].to_broadcast([P, P]), identb[:])
            (pgs, pbs)[w][e] = dst

        mask = cst.tile([P, GB], F32, name="mask")
        nc.vector.tensor_reduce(out=mask[:], in_=ident[:].rearrange("p (b n) -> p b n", n=NA), axis=AX.X, op=ALU.add)
        lgf = cst.tile([P, G, E], F32, name="lgf")
        nc.vector.tensor_copy(out=lgf[:], in_=lg_raw[:, :, 0:E])
        psT = psH.tile([P, GB, NA], F32, tag="ph", name="psT")
        nc.tensor.transpose(psT[:].rearrange("p b n -> p (b n)"), lgf[:].rearrange("p g e -> p (g e)"), ident[:])
        mx = cst.tile([P, GB], F32, name="mx")
        nc.vector.tensor_reduce(out=mx[:], in_=psT[:], axis=AX.X, op=ALU.max)
        sh = cst.tile([P, GB, NA], F32, name="sh")
        nc.vector.tensor_tensor(out=sh[:], in0=psT[:], in1=mx[:].unsqueeze(2).to_broadcast([P, GB, NA]), op=ALU.subtract)
        nc.scalar.activation(out=sh[:], in_=sh[:], func=ACT.Exp)
        dn = cst.tile([P, 2, NV, NA], F32, name="dn")
        dnv = dn[:].rearrange("b t e n -> b (t e) n")
        nc.vector.tensor_copy(out=dn[:], in_=lgn[:].rearrange("b t (n e) -> b t e n", e=E)[:, :, EP:E, :])
        mxn = cst.tile([P, 2 * NV], F32, name="mxn")
        nc.vector.tensor_reduce(out=mxn[:], in_=dnv, axis=AX.X, op=ALU.max)
        sm = cst.tile([P, GB], F32, name="sm")
        nc.vector.tensor_reduce(out=sm[:], in_=sh[:], axis=AX.X, op=ALU.add)
        rs = cst.tile([P, GB], F32, name="rs")
        nc.vector.reciprocal(out=rs[:], in_=sm[:])
        nc.vector.tensor_tensor(out=dnv, in0=dnv, in1=mxn[:].unsqueeze(2).to_broadcast([P, 2 * NV, NA]), op=ALU.subtract)
        nc.scalar.activation(out=dnv, in_=dnv, func=ACT.Exp)
        nc.vector.tensor_tensor(out=sh[:], in0=sh[:], in1=rs[:].unsqueeze(2).to_broadcast([P, GB, NA]), op=ALU.mult)
        psD = psH.tile([P, G, E], F32, tag="ph", name="psD")
        nc.tensor.transpose(psD[:].rearrange("p g e -> p (g e)"), sh[:].rearrange("p b n -> p (b n)"), ident[:])

        smn = cst.tile([P, 2 * NV], F32, name="smn")
        rsn = cst.tile([P, 2 * NV], F32, name="rsn")

        def normalise_by_batch():
            nc.vector.tensor_reduce(out=smn[:], in_=dnv, axis=AX.X, op=ALU.add)
            nc.vector.reciprocal(out=rsn[:], in_=smn[:])
            nc.vector.tensor_tensor(out=dnv, in0=dnv, in1=rsn[:].unsqueeze(2).to_broadcast([P, 2 * NV, NA]), op=ALU.mult)

        psR = psH.tile([P, P], BF16, tag="ph", name="psR")
        nc.tensor.transpose(psR[:], rows[:], identb[:])

        tfs = []
        for q in range(4):
            tf = xp.tile([P, 4, PACK, P], F32, tag="x", name="tf%d" % q)
            tfs.append(tf)

        def pool_copy(out, in_):
            nc.gpsimd.tensor_scalar(out=out, in0=in_, scalar1=1.0, scalar2=0.0, op0=ALU.mult, op1=ALU.add)

        def cast(q):
            copy_fn = {"V": nc.vector.tensor_copy, "S": nc.scalar.copy, "G": pool_copy}[CB[q]]
            copy_fn(out=tfs[q][:], in_=trs[q][:].rearrange("p i (q j) -> p i j q", j=PACK))

        dblk = cst.tile([P, G, EP, GB], F32, name="dblk")

        def spread_dispatch(g0, n):
            nc.vector.tensor_tensor(
                out=dblk[:, g0:g0 + n, :, :],
                in0=psD[:, g0:g0 + n, 0:EP].unsqueeze(3).to_broadcast([P, n, EP, GB]),
                in1=mask[:].unsqueeze(1).unsqueeze(1).to_broadcast([P, n, EP, GB]),
                op=ALU.mult,
            )

        spread_dispatch(0, 4)
        cast(0)
        cast(1)
        spread_dispatch(4, 12)
        cast(2)
        cast(3)
        gcol = cst.tile([P, P], BF16, name="gcol")
        nc.vector.tensor_copy(out=gcol[:], in_=psR[:])

        wgs = {}

        def regroup(e):
            wgs[e] = wgp.tile([P, H, PACK], BF16, tag="wg", name="wg%d" % e, align_bytes=64)
            pieces = [(pool_copy, c0, c0 + GP) for c0 in range(0, H, GP)] if RB[e] == "G" else [(nc.vector.tensor_copy, 0, HS[e])] + [(nc.scalar.copy, c0, c0 + SP) for c0 in range(HS[e], H, SP)]
            for copy_fn, c0, c1 in pieces:
                if c0 < c1:
                    copy_fn(
                        out=wgs[e][:, c0:c1, :].rearrange("p (c i) t -> p c t i", i=4),
                        in_=wrs[e][:, :, c0:c1].rearrange("p t (c i) -> p c t i", i=4),
                    )
            if e + 3 < E:
                load_weights(e + 3)

        def quantise_weights(e):
            wcs[e] = wcp.tile([P, H], U32, tag="wc", name="wc%d" % e, align_bytes=64)
            wss[e] = wcp.tile([P, H], U8, tag="ws", name="ws%d" % e, align_bytes=64)
            nc.vector.quantize_mx(
                out=wcs[e][:].bitcast(FP8X4), scales=wss[e][:], in_=wgs[e][:].rearrange("p h j -> p (h j)")
            )

        gs = cst.tile([P, E, B, PACK], BF16, name="gs", align_bytes=64)
        sc = cst.tile([P, E, B], U32, name="sc", align_bytes=64)
        ss = cst.tile([P, E, B], U8, name="ss", align_bytes=64)

        def quantise_slots(e0, e1):
            nc.vector.quantize_mx(
                out=sc[:, e0:e1, :].rearrange("p e b -> p (e b)").bitcast(FP8X4),
                scales=ss[:, e0:e1, :].rearrange("p e b -> p (e b)"),
                in_=gs[:, e0:e1, :, :].rearrange("p e b j -> p (e b j)"),
            )

        prods = {}

        def product(t, i, n, by):
            if n % 4 == 0:
                prods[(t, i, n // 4)] = (xp if t * i else up).tile([P, 4, PACK, P], F32, tag="x" if t * i else "u", name="prod%d_%d_%d" % (t, i, n // 4))
            dst, src = prods[(t, i, n // 4)][:, n % 4, :, :], tns[t][:, n, :].rearrange("p (q j) -> p j q", j=PACK)
            if by == "G":
                nc.gpsimd.tensor_scalar(out=dst, in0=src, scalar1=dn[:, t, i, n:n + 1], scalar2=0.0, op0=ALU.mult, op1=ALU.add)
            elif by == "S":
                nc.scalar.activation(out=dst, in_=src, func=ACT.Copy, scale=dn[:, t, i, n:n + 1])
            else:
                nc.vector.tensor_scalar_mul(out=dst, in0=src, scalar1=dn[:, t, i, n:n + 1])

        psts = {}

        def sum_products(t, i):
            psts[(t, i)] = psH.tile([P, PACK, P], F32, tag="ph", name="pst%d_%d" % (t, i))
            for j in range(PACK):
                for n in range(NA):
                    nc.tensor.matmul(
                        psts[(t, i)][:, j, :], lhsT=prods[(t, i, n // 4)][:, n % 4, j, :], rhs=ident[:],
                        start=(n == 0), stop=(n == NA - 1), is_transpose=True,
                    )

        def store_sums(t, i):
            nc.scalar.copy(out=gs[:, EP + i, P * t:P * t + P, :], in_=psts[(t, i)][:].rearrange("p j b -> p b j"))

        xs, us, sums, negmus, vss, rstds, mvs, phs = {}, {}, {}, {}, {}, {}, {}, {}
        junk = cst.tile([P, H], BF16, name="junk")
        out_v = out.rearrange("(t b) e h -> b t e h", b=P)

        def multiply(e):
            for t in range(2):
                for hh in range(2):
                    phs[(e, t, hh)] = psH.tile([P, 512], F32, tag="ph", name="ph%d_%d_%d" % (e, t, hh))
                    nc.tensor.matmul_mx(
                        out=phs[(e, t, hh)][:],
                        lhsT=sc[:, e, P * t:P * t + P].bitcast(FP8X4),
                        lhsT_scale=ss[:, e, P * t:P * t + P],
                        rhs=wcs[e][:, 512 * hh:512 * hh + 512].bitcast(FP8X4),
                        rhs_scale=wss[e][:, 512 * hh:512 * hh + 512],
                        start=True,
                        stop=True,
                    )

        s01s, st6s = {}, {}

        def add_bias(e):
            by_scalar = e in BY_SCALAR
            xs[e] = xp.tile([P, 2, H], F32, tag="x", name="x%d" % e)
            if by_scalar:
                s01s[e] = stp.tile([P, 2, 2], F32, tag="s01", name="s01_%d" % e)
                sums[e] = stp.tile([P, 2], F32, tag="sum", name="sum%d" % e)
            for t in range(2):
                for hh in range(2):
                    nc.vector.scalar_tensor_tensor(
                        out=xs[e][:, t, 512 * hh:512 * hh + 512],
                        in0=phs[(e, t, hh)][:],
                        scalar=1.0,
                        in1=bb[:, e, 512 * hh:512 * hh + 512],
                        op0=ALU.mult,
                        op1=ALU.add,
                        accum_out=s01s[e][:, t, hh:hh + 1] if by_scalar else None,
                    )
                    if by_scalar and (t, hh) == (1, 0):
                        add_halves(e, 0)
            if not by_scalar:
                st6s[e] = stp.tile([P, 2, 2, 6], F32, tag="st6", name="st6_%d" % e)
                mvs[e] = stp.tile([P, 2, 2], F32, tag="mv", name="mv%d" % e)
                for t in range(2):
                    for hh in range(2):
                        nc.vector.bn_stats(out=st6s[e][:, t, hh, :], in_=xs[e][:, t, 512 * hh:512 * hh + 512])
                        if (t, hh) == (1, 0):
                            add_halves(e, 0)

        def add_halves(e, t):
            if e in BY_SCALAR:
                nc.vector.tensor_reduce(out=sums[e][:, t:t + 1], in_=s01s[e][:, t, :], axis=AX.X, op=ALU.add)
            else:
                nc.vector.bn_aggr(out=mvs[e][:, t, :], in_=st6s[e][:, t, :, :].rearrange("p a s -> p (a s)"))

        def statistics(e):
            rstds[e] = stp.tile([P, 2], F32, tag="rstd", name="rstd%d" % e)
            ve = stp.tile([P, 2], F32, tag="ve", name="ve%d" % e)
            if e in BY_SCALAR:
                negmus[e] = stp.tile([P, 2], F32, tag="negmu", name="negmu%d" % e)
                nc.gpsimd.tensor_scalar(out=negmus[e][:], in0=sums[e][:], scalar1=-1.0 / H, scalar2=0.0, op0=ALU.mult, op1=ALU.add)
                vss[e] = stp.tile([P, 2], F32, tag="vs", name="vs%d" % e)
                for t in range(2):
                    nc.scalar.activation(
                        out=junk[:], in_=xs[e][:, t, :], func=ACT.Square, scale=-1.0 * H, bias=sums[e][:, t:t + 1],
                        accum_out=vss[e][:, t:t + 1],
                    )
                nc.gpsimd.tensor_scalar(out=ve[:], in0=vss[e][:], scalar1=1.0 / H ** 3, scalar2=EPS, op0=ALU.mult, op1=ALU.add)
            else:
                nc.gpsimd.tensor_scalar(out=ve[:], in0=mvs[e][:, :, 1], scalar1=1.0, scalar2=EPS, op0=ALU.mult, op1=ALU.add)
            nc.gpsimd.tensor_tensor(out=rstds[e][:], in0=ve[:], in1=mhalf[:, 0:2], op=ALU.pow)

        def centre_times_gamma(e):
            for t in range(2):
                nc.vector.scalar_tensor_tensor(
                    out=xs[e][:, t, :], in0=xs[e][:, t, :],
                    scalar=negmus[e][:, t:t + 1] if e in BY_SCALAR else mvs[e][:, t, 0:1], in1=pgs[e][:],
                    op0=ALU.add if e in BY_SCALAR else ALU.subtract, op1=ALU.mult,
                )
            spread(0, e + 1)

        def scale_add_beta(e):
            for t in range(2):
                nc.vector.scalar_tensor_tensor(
                    out=xs[e][:, t, :], in0=xs[e][:, t, :], scalar=rstds[e][:, t:t + 1], in1=pbs[e][:],
                    op0=ALU.mult, op1=ALU.add,
                )
            spread(1, e + 1)

        def flat(tl):
            return tl[:].rearrange("p t h -> p (t h)")

        def exponential(e):
            us[e] = up.tile([P, 2, H], F32, tag="u", name="u%d" % e)
            for t in range(2):
                nc.scalar.activation(out=us[e][:, t, :], in_=xs[e][:, t, :], func=ACT.Exp)

        def logarithm(e):
            nc.scalar.activation(out=flat(us[e]), in_=flat(us[e]), func=ACT.Ln, bias=1.0)

        def finish(e):
            tanh_only(e)
            multiply_store(e)

        def tanh_only(e):
            pieces = 2 if e == E - 1 else 1
            w = H // pieces
            if e == E - 1:
                return
            for t in range(2):
                nc.scalar.activation(out=us[e][:, t, :], in_=us[e][:, t, :], func=ACT.Tanh)

        def multiply_store(e):
            eng = nc.gpsimd if e in BY_POOL else nc.vector
            pieces = 2 if e == E - 1 else 1
            w = H // pieces
            for t in range(2):
                for d in range(pieces):
                    cs = slice(d * w, (d + 1) * w)
                    if e == E - 1:
                        nc.scalar.activation(out=us[e][:, t, cs], in_=us[e][:, t, cs], func=ACT.Tanh)
                    eng.tensor_tensor(out=us[e][:, t, cs], in0=xs[e][:, t, cs], in1=us[e][:, t, cs], op=ALU.mult)
                    nc.sync.dma_start(out=out_v[:, t, e, cs], in_=us[e][:, t, cs])

        def slot_group(g):
            ps = psH.tile([P, PACK, EP * GB], F32, tag="ph", name="ps%d" % g)
            for j in range(PACK):
                nc.tensor.matmul(
                    ps[:, j, :],
                    lhsT=tfs[g // 4][:, g % 4, j, :],
                    rhs=dblk[:, g, :, :].rearrange("p e b -> p (e b)"),
                    start=True,
                    stop=True,
                )
            nc.scalar.copy(out=gs[:, 0:EP, GB * g:GB * g + GB, :], in_=ps[:].rearrange("p j (e b) -> p e b j", e=EP))

        NBT = len(BATCHES)

        def batch(c):
            return BATCHES[c] if 0 <= c < NBT else ()

        order = [(0, i, n) for i in range(NV) for n in range(NA)]
        for g in range(G):
            slot_group(g)
            if g == 0:
                normalise_by_batch()
                regroup(0)
                load_bias(0)
            if g == 5:
                quantise_weights(0)
                regroup(1)
            if g == 8:
                quantise_weights(1)
                regroup(2)
            for step in order[PS[g]:PS[g + 1]]:
                product(*step, PB[0])
        for step in order[PS[G]:]:
            product(*step, PB[0])
        quantise_weights(2)
        for i in range(NV):
            for n in range(NA):
                product(1, i, n, "V")
        load_bias(1)
        quantise_slots(0, 2)
        regroup(3)
        multiply(0)
        spread(0, 0)
        spread(1, 0)
        add_bias(0)
        multiply(1)
        quantise_slots(2, 4)
        add_halves(0, 1)
        statistics(0)
        add_bias(1)
        sum_products(0, 0)
        quantise_slots(4, 6)
        add_halves(1, 1)
        statistics(1)
        store_sums(0, 0)
        sum_products(0, 1)
        sum_products(1, 0)
        store_sums(0, 1)
        for e in REGROUPS[-1]:
            regroup(e)
        pending = []
        for c in range(NBT):
            for k in batch(c):
                if k + AHEAD < E:
                    multiply(k + AHEAD)
                centre_times_gamma(k)
                scale_add_beta(k)
                exponential(k)
                for e in REGROUPS.get(k, ()):
                    regroup(e)
                if k == 0:
                    store_sums(1, 0)
                if k + AHEAD < E:
                    add_bias(k + AHEAD)
                    if k + PREP < E:
                        quantise_weights(k + PREP)
                    add_halves(k + AHEAD, 1)
                    statistics(k + AHEAD)
                while pending:
                    multiply_store(pending.pop(0))
                for e in LATER.get(k, ()):
                    regroup(e)
                if k == 0:
                    sum_products(1, 1)
                if k == 1:
                    store_sums(1, 1)
                if k == 2:
                    quantise_slots(6, 8)
            for k in batch(c):
                logarithm(k)
            for k in batch(c):
                tanh_only(k)
                if k == batch(c)[0] or c == NBT - 1:
                    multiply_store(k)
                else:
                    pending.append(k)
